import numpy as np
import ml_dtypes


def mxq(x, axis, fmt="e4m3"):
    dtype, down = {"e4m3": (ml_dtypes.float8_e4m3fn, 7), "e5m2": (ml_dtypes.float8_e5m2, 14)}[fmt]
    v = np.moveaxis(np.asarray(x, np.float32).astype(ml_dtypes.bfloat16).astype(np.float64), axis, -1)
    blocks = v.reshape(v.shape[:-1] + (-1, 32))
    amax = np.abs(blocks).max(-1, keepdims=True)
    byte = np.maximum(np.where(amax > 0, np.frexp(amax)[1] - 1 + 127, 0) - down, 1)
    scale = np.exp2(byte - 127.0)
    codes = (blocks / scale).astype(np.float32).astype(dtype).astype(np.float64)
    return np.moveaxis((codes * scale).reshape(v.shape), -1, axis)


WIDE = False


def mx_kscale(k):
    if not WIDE:
        return np.ones(k)
    levels = np.array([10, -10, 5, -5, 0])
    if k % 512:
        return np.exp2(np.random.permutation(np.resize(levels, k // 32))).repeat(32)
    a = np.empty((k // 512, 16))
    for p in range(k // 512):
        a[p, :8] = np.random.permutation(np.resize(levels, 8))
        for g in range(8):
            far = levels[np.abs(levels - a[p, g]) >= 10]
            a[p, g + 8] = far[np.random.randint(len(far))]
    return np.exp2(a.ravel()).repeat(32)


BF16 = ml_dtypes.bfloat16


def bf(x):
    return np.asarray(x, np.float32).astype(BF16)


def f64(x):
    return np.asarray(x).astype(np.float64)


B, F, L, SEG, PRED, D, H = 16, 128, 48, 24, 192, 512, 256
R = B * F
T = PRED // SEG
EPS = 1e-15
MAXN = 1.0 - 1e-5


def norm(a):
    return np.sqrt(np.maximum(np.sum(a * a, axis=-1, keepdims=True), EPS))


def artanh(r):
    c = np.clip(r, -1.0 + 1e-7, 1.0 - 1e-7)
    return 0.5 * np.log((1.0 + c) / (1.0 - c))


def projx(a):
    n = norm(a)
    return np.where(n > MAXN, a * (MAXN / n), a)


def mobius_add(x, y):
    x2 = np.sum(x * x, -1, keepdims=True)
    y2 = np.sum(y * y, -1, keepdims=True)
    xy = np.sum(x * y, -1, keepdims=True)
    num = (1.0 + 2.0 * xy + y2) * x + (1.0 - x2) * y
    den = 1.0 + 2.0 * xy + x2 * y2
    return num / np.maximum(den, EPS)


def lam(x):
    return 2.0 / np.maximum(1.0 - np.sum(x * x, -1, keepdims=True), EPS)


def expmap(x, v):
    n = norm(v)
    second = np.tanh(lam(x) * n / 2.0) * v / n
    return projx(mobius_add(x, second))


def logmap0(x):
    n = norm(x)
    return artanh(n) * x / n


def setup_inputs():
    s = mx_kscale(D)
    c = np.exp2(np.ceil(np.log2(np.sqrt(np.mean(s * s)))))
    return {"z0": bf(np.random.standard_normal((R, D)) * 0.46 / np.sqrt(D) * s / c),
            "v0t": bf(np.random.standard_normal((R, D)) * 0.79 / np.sqrt(D) * s / c),
            "step_sizes": bf(-1.5 + 0.1 * np.random.standard_normal(1)),
            "W1": bf(np.random.standard_normal((D, H)) * c / s[:, None]),
            "b1": bf(np.random.standard_normal(H) * 0.3)}


def reference(z0, v0t, step_sizes, W1, b1):
    step = 1.0 / (1.0 + np.exp(-f64(step_sizes)))
    t_vals = np.arange(1, T + 1) * 1.0
    v_all = step * t_vals[None, :, None] * f64(v0t)[:, None, :]
    z_fut = expmap(f64(z0)[:, None, :], v_all)
    tan = logmap0(z_fut)
    return np.maximum((mxq(tan, 2, "e4m3") @ mxq(f64(W1), 0, "e4m3")) + f64(b1), 0.0)

@@ -1,0 +1,371 @@
+import math
+from contextlib import ExitStack
+
+import concourse.mybir as mybir
+from concourse.masks import make_identity
+
+F32 = mybir.dt.float32
+BF16 = mybir.dt.bfloat16
+U32 = mybir.dt.uint32
+U8 = mybir.dt.uint8
+FP8X4 = mybir.dt.float8_e4m3fn_x4
+ACT = mybir.ActivationFunctionType
+ALU = mybir.AluOpType
+
+P = 128
+ROWS = 2048
+D = 512
+STEPS = 8
+H = 256
+ROW_TILES = ROWS // P
+HALF = STEPS // 2
+WORDS = D // 2
+H_TILES = H // P
+FIRST_TILES = 4
+HALVES = 2 * ROW_TILES
+BANKS = 2 * HALVES
+MX_REPEATS = 2
+
+EPS = 1e-15
+MAXN = 1.0 - 1e-5
+TINY = 1e-30
+
+FLOPS = 2 * ROWS * STEPS * D * H
+
+
+def tile_directnodecomphyperbolicforecaster_pb_t_kernel(tc, z0, v0t, step_sizes, W1, b1, out):
+    nc = tc.nc
+    z0_rows = z0.rearrange("(p i) d -> p i d", i=ROW_TILES)
+    v0_rows = v0t.rearrange("(p i) d -> p i d", i=ROW_TILES)
+    out_rows = out.rearrange("(p i) t h -> p i t h", i=ROW_TILES)
+
+    with ExitStack() as ctx:
+        consts = ctx.enter_context(tc.tile_pool(name="consts", bufs=1))
+        coef = ctx.enter_context(tc.tile_pool(name="coef", bufs=1))
+        unread = ctx.enter_context(tc.tile_pool(name="unread", bufs=4))
+        stream = ctx.enter_context(tc.tile_pool(name="stream", bufs=3))
+        psum_v0 = ctx.enter_context(tc.psum_pool(name="psum_v0", bufs=2))
+        psum_in = ctx.enter_context(tc.psum_pool(name="psum_in", bufs=2))
+        psum_mm = ctx.enter_context(tc.psum_pool(name="psum_mm", bufs=2))
+        psum_out = ctx.enter_context(tc.psum_pool(name="psum_out", bufs=2))
+
+        z0_sb = consts.tile([P, ROW_TILES, D], BF16)
+        v0_sb = consts.tile([P, ROW_TILES, D], BF16)
+        raw_step = consts.tile([P, 1], BF16)
+        w_raw = consts.tile([P, 4, H], BF16)
+        b_rows = consts.tile([P, P], BF16)
+        nc.vector.memset(b_rows[:], 0.0)
+        nc.sync.dma_start(out=raw_step[:], in_=step_sizes.partition_broadcast(P))
+        for first in range(0, ROW_TILES, FIRST_TILES):
+            tiles = slice(first, first + FIRST_TILES)
+            nc.sync.dma_start(out=z0_sb[:, tiles, :], in_=z0_rows[:, tiles, :])
+            nc.sync.dma_start(out=v0_sb[:, tiles, :], in_=v0_rows[:, tiles, :])
+            if first == 0:
+                nc.sync.dma_start(out=w_raw[:], in_=W1.rearrange("(q j) c -> q j c", j=4))
+                nc.sync.dma_start(out=b_rows[0:H_TILES, :], in_=b1.rearrange("(c h) -> c h", c=H_TILES))
+
+        warm = consts.tile([P, 1], F32)
+        nc.vector.memset(warm[:], 1.0)
+        nc.scalar.activation(out=warm[:], in_=warm[:], func=ACT.Sqrt)
+
+        ident = consts.tile([P, P], F32)
+        make_identity(nc, ident[:])
+        ident_bf16 = consts.tile([P, P], BF16)
+        make_identity(nc, ident_bf16[:])
+
+        step_number = consts.tile([P, STEPS], F32)
+        for t in range(STEPS):
+            nc.vector.memset(step_number[:, t : t + 1], float(t + 1))
+
+        w_grouped = consts.tile([P, H, 4], BF16, align_bytes=64)
+        w_codes = consts.tile([P, H], U32, align_bytes=64)
+        w_scales = consts.tile([P, H], U8, align_bytes=64)
+        nc.vector.tensor_copy(out=w_grouped[:], in_=w_raw[:].rearrange("p j c -> p c j"))
+
+        b_rows32 = consts.tile([P, P], F32)
+        b_col = consts.tile([P, H_TILES], F32)
+        nc.vector.tensor_copy(out=b_rows32[:], in_=b_rows[:])
+        b_turned = psum_in.tile([P, P], F32, tag="turned")
+        nc.tensor.transpose(out=b_turned[:], in_=b_rows32[:], identity=ident[:])
+        nc.vector.tensor_copy(out=b_col[:], in_=b_turned[:, 0:H_TILES])
+        nc.vector.quantize_mx(
+            out=w_codes[:].bitcast(FP8X4), scales=w_scales[:], in_=w_grouped[:].rearrange("p c j -> p (c j)")
+        )
+
+        x2 = coef.tile([P, ROW_TILES], F32)
+        vv = coef.tile([P, ROW_TILES], F32)
+        xv = coef.tile([P, ROW_TILES], F32)
+
+        def scalar_sum_of_squares(x, total):
+            squares = unread.tile([P, D], BF16)
+            nc.scalar.activation(out=squares[:], in_=x, func=ACT.Square, accum_out=total)
+
+        def vector_sum_of_products(x, y, total):
+            products = unread.tile([P, D], F32)
+            nc.vector.scalar_tensor_tensor(
+                out=products[:], in0=x, scalar=1.0, in1=y, op0=ALU.mult, op1=ALU.mult, accum_out=total
+            )
+
+        def row_sums(i):
+            z_i, v_i = z0_sb[:, i, :], v0_sb[:, i, :]
+            scalar_sum_of_squares(z_i, x2[:, i : i + 1])
+            vector_sum_of_products(z_i, v_i, xv[:, i : i + 1])
+            if i < ROW_TILES // 2:
+                vector_sum_of_products(v_i, v_i, vv[:, i : i + 1])
+            else:
+                scalar_sum_of_squares(v_i, vv[:, i : i + 1])
+
+        def row_tile(name):
+            return coef.tile([P, ROW_TILES], F32, name=name)
+
+        def grid_tile(name):
+            return coef.tile([P, ROW_TILES, STEPS], F32, name=name)
+
+        step = consts.tile([P, 1], F32)
+        step_t = consts.tile([P, STEPS], F32)
+        step_t_capped = consts.tile([P, STEPS], F32)
+        one_minus_x2 = row_tile("one_minus_x2")
+        half_lambda = row_tile("half_lambda")
+        vv_floor = row_tile("vv_floor")
+        root_vv = row_tile("root_vv")
+        newton_row = row_tile("newton_row")
+        inv_root_vv = row_tile("inv_root_vv")
+        norm_v = grid_tile("norm_v")
+        tanh_arg = grid_tile("tanh_arg")
+        tanh_val = grid_tile("tanh_val")
+        y_over_v = grid_tile("y_over_v")
+        xy = grid_tile("xy")
+        y2 = grid_tile("y2")
+        two_xy_y2 = grid_tile("two_xy_y2")
+        den = grid_tile("den")
+        inv_den = grid_tile("inv_den")
+        norm2_m = grid_tile("norm2_m")
+        norm_m = grid_tile("norm_m")
+        newton = grid_tile("newton")
+        inv_norm_m = grid_tile("inv_norm_m")
+        norm_z = grid_tile("norm_z")
+        one_plus = grid_tile("one_plus")
+        one_minus = grid_tile("one_minus")
+        log_ratio = grid_tile("log_ratio")
+        gain = grid_tile("gain")
+        gain_z = grid_tile("gain_z")
+        gain_v = grid_tile("gain_v")
+        alpha = grid_tile("alpha")
+        beta = grid_tile("beta")
+
+        def load_table_of(func, after):
+            nc.scalar.activation(out=warm[:], in_=after, func=func)
+
+        def step_sizes_times_t():
+            nc.scalar.activation(out=step[:], in_=raw_step[:], func=ACT.Tanh, scale=0.5)
+            nc.vector.tensor_scalar(out=step[:], in0=step[:], scalar1=0.5, scalar2=0.5, op0=ALU.mult, op1=ALU.add)
+            nc.vector.tensor_scalar(out=step_t[:], in0=step_number[:], scalar1=step[:, 0:1], scalar2=None, op0=ALU.mult)
+            nc.vector.tensor_scalar(
+                out=step_t_capped[:], in0=step_t[:], scalar1=1.0 / math.sqrt(EPS), scalar2=None, op0=ALU.mult
+            )
+
+        def coefficients(first, count, with_step):
+            shape = [P, count, STEPS]
+            v = nc.vector
+
+            def rows(x):
+                return x[:, first : first + count]
+
+            def grid(x):
+                return x[:, first : first + count, :]
+
+            def over_steps(x):
+                return rows(x).unsqueeze(2).to_broadcast(shape)
+
+            def over_rows(x):
+                return x[:].unsqueeze(1).to_broadcast(shape)
+
+            v.tensor_scalar(out=rows(one_minus_x2), in0=rows(x2), scalar1=-1.0, scalar2=1.0, op0=ALU.mult, op1=ALU.add)
+            v.tensor_scalar_max(out=rows(half_lambda), in0=rows(one_minus_x2), scalar1=EPS)
+            v.reciprocal(out=rows(half_lambda), in_=rows(half_lambda))
+            v.tensor_scalar_max(out=rows(vv_floor), in0=rows(vv), scalar1=TINY)
+            nc.scalar.activation(out=rows(root_vv), in_=rows(vv_floor), func=ACT.Sqrt)
+            load_table_of(ACT.Tanh, root_vv[:, first : first + 1])
+            v.reciprocal(out=rows(newton_row), in_=rows(root_vv))
+            v.scalar_tensor_tensor(
+                out=rows(newton_row), in0=rows(vv_floor), scalar=0.5, in1=rows(newton_row), op0=ALU.mult, op1=ALU.mult
+            )
+            v.scalar_tensor_tensor(
+                out=rows(root_vv), in0=rows(root_vv), scalar=0.5, in1=rows(newton_row), op0=ALU.mult, op1=ALU.add
+            )
+            v.reciprocal(out=rows(inv_root_vv), in_=rows(root_vv))
+            if with_step:
+                step_sizes_times_t()
+            v.tensor_tensor(out=grid(norm_v), in0=over_steps(root_vv), in1=over_rows(step_t), op=ALU.mult)
+            v.scalar_tensor_tensor(
+                out=grid(tanh_arg), in0=grid(norm_v), scalar=math.sqrt(EPS), in1=over_steps(half_lambda),
+                op0=ALU.max, op1=ALU.mult,
+            )
+            nc.scalar.activation(out=grid(tanh_val), in_=grid(tanh_arg), func=ACT.Tanh)
+            load_table_of(ACT.Sqrt, tanh_val[:, first, 0:1])
+            v.tensor_tensor(out=grid(y_over_v), in0=over_steps(inv_root_vv), in1=over_rows(step_t_capped), op=ALU.min)
+            v.tensor_mul(out=grid(y_over_v), in0=grid(y_over_v), in1=grid(tanh_val))
+            v.tensor_tensor(out=grid(xy), in0=grid(y_over_v), in1=over_steps(xv), op=ALU.mult)
+            v.tensor_tensor(out=grid(y2), in0=grid(y_over_v), in1=over_steps(vv), op=ALU.mult)
+            v.tensor_mul(out=grid(y2), in0=grid(y2), in1=grid(y_over_v))
+            v.scalar_tensor_tensor(
+                out=grid(two_xy_y2), in0=grid(xy), scalar=2.0, in1=grid(y2), op0=ALU.mult, op1=ALU.add
+            )
+            v.tensor_tensor(out=grid(den), in0=grid(y2), in1=over_steps(x2), op=ALU.mult)
+            v.scalar_tensor_tensor(out=grid(den), in0=grid(xy), scalar=2.0, in1=grid(den), op0=ALU.mult, op1=ALU.add)
+            v.tensor_scalar(out=grid(den), in0=grid(den), scalar1=1.0, scalar2=EPS, op0=ALU.add, op1=ALU.max)
+            v.reciprocal(out=grid(inv_den), in_=grid(den))
+            v.tensor_tensor(out=grid(norm2_m), in0=grid(two_xy_y2), in1=over_steps(x2), op=ALU.add)
+            v.tensor_mul(out=grid(norm2_m), in0=grid(norm2_m), in1=grid(inv_den))
+            v.tensor_scalar_max(out=grid(norm2_m), in0=grid(norm2_m), scalar1=EPS)
+            nc.scalar.activation(out=grid(norm_m), in_=grid(norm2_m), func=ACT.Sqrt)
+            load_table_of(ACT.Ln, norm2_m[:, first, 0:1])
+            v.reciprocal(out=grid(newton), in_=grid(norm_m))
+            v.scalar_tensor_tensor(
+                out=grid(newton), in0=grid(norm2_m), scalar=0.5, in1=grid(newton), op0=ALU.mult, op1=ALU.mult
+            )
+            v.scalar_tensor_tensor(
+                out=grid(norm_m), in0=grid(norm_m), scalar=0.5, in1=grid(newton), op0=ALU.mult, op1=ALU.add
+            )
+            v.tensor_scalar_min(out=grid(norm_z), in0=grid(norm_m), scalar1=MAXN)
+            v.tensor_scalar(out=grid(one_minus), in0=grid(norm_z), scalar1=-1.0, scalar2=1.0, op0=ALU.mult, op1=ALU.add)
+            v.reciprocal(out=grid(one_minus), in_=grid(one_minus))
+            v.tensor_scalar_add(out=grid(one_plus), in0=grid(norm_z), scalar1=1.0)
+            v.tensor_mul(out=grid(one_plus), in0=grid(one_plus), in1=grid(one_minus))
+            nc.scalar.activation(out=grid(log_ratio), in_=grid(one_plus), func=ACT.Ln)
+            load_table_of(ACT.Sqrt, one_plus[:, first, 0:1])
+            v.reciprocal(out=grid(inv_norm_m), in_=grid(norm_m))
+            v.tensor_mul(out=grid(gain), in0=grid(inv_norm_m), in1=grid(inv_den))
+            v.scalar_tensor_tensor(
+                out=grid(gain_z), in0=grid(two_xy_y2), scalar=1.0, in1=grid(gain), op0=ALU.add, op1=ALU.mult
+            )
+            v.tensor_mul(out=grid(gain_v), in0=grid(y_over_v), in1=grid(gain))
+            v.tensor_tensor(out=grid(gain_v), in0=grid(gain_v), in1=over_steps(one_minus_x2), op=ALU.mult)
+            v.scalar_tensor_tensor(
+                out=grid(alpha), in0=grid(log_ratio), scalar=0.5, in1=grid(gain_z), op0=ALU.mult, op1=ALU.mult
+            )
+            v.scalar_tensor_tensor(
+                out=grid(beta), in0=grid(log_ratio), scalar=0.5, in1=grid(gain_v), op0=ALU.mult, op1=ALU.mult
+            )
+
+        for i in range(FIRST_TILES):
+            row_sums(i)
+        coefficients(0, FIRST_TILES, True)
+        for i in range(FIRST_TILES, ROW_TILES):
+            row_sums(i)
+        coefficients(FIRST_TILES, ROW_TILES - FIRST_TILES, False)
+
+        scaled_z, v0_psum, tan, turned, grouped, codes, scales = {}, {}, {}, {}, {}, {}, {}
+        acc, hidden, back, result = {}, {}, {}, {}
+
+        def scale(s):
+            i = s // 2
+            scaled_z[s] = []
+            for q in range(HALF):
+                t = (s % 2) * HALF + q
+                scaled = stream.tile([P, D], F32, bufs=2 * HALF)
+                nc.gpsimd.tensor_scalar(
+                    out=scaled[:], in0=z0_sb[:, i, :], scalar1=alpha[:, i, t : t + 1], scalar2=0.0,
+                    op0=ALU.mult, op1=ALU.add,
+                )
+                scaled_z[s].append(scaled)
+
+        def copy_v0(i):
+            v0_psum[i] = psum_v0.tile([P, D], F32, name="v0_copy")
+            nc.tensor.matmul(out=v0_psum[i][:], lhsT=ident_bf16[:], rhs=v0_sb[:, i, :], start=True, stop=True)
+
+        def combine(s):
+            i = s // 2
+            tan[s] = stream.tile([P, HALF * D], BF16, name="tan")
+            for q in range(HALF):
+                t = (s % 2) * HALF + q
+                nc.vector.scalar_tensor_tensor(
+                    out=tan[s][:, q * D : (q + 1) * D], in0=v0_psum[i][:], scalar=beta[:, i, t : t + 1],
+                    in1=scaled_z[s][q][:], op0=ALU.mult, op1=ALU.add,
+                )
+
+        def turn_in(m):
+            s, pair = divmod(m, 2)
+            tan_words = tan[s][:].bitcast(F32)
+            turned[m] = psum_in.tile([P, 2, 2 * P], F32, name="turned", tag="turned")
+            for q in range(2):
+                for u in range(2):
+                    first_word = (2 * pair + q) * WORDS
+                    nc.tensor.transpose(
+                        out=turned[m][:, u, q * P : (q + 1) * P],
+                        in_=tan_words[:, first_word + u : first_word + WORDS : 2],
+                        identity=ident[:],
+                    )
+
+        def gather(m):
+            s, pair = divmod(m, 2)
+            if pair == 0:
+                grouped[s] = stream.tile([P, HALF * P * 4], BF16, name="grouped", align_bytes=64)
+            grouped_words = grouped[s][:].bitcast(F32).rearrange("p (c u) -> p c u", u=2)
+            nc.scalar.copy(
+                out=grouped_words[:, pair * 2 * P : (pair + 1) * 2 * P, :],
+                in_=turned[m][:].rearrange("p u c -> p c u"),
+            )
+
+        def quantise(s):
+            codes[s] = stream.tile([P, HALF * P], U32, name="codes", align_bytes=64)
+            scales[s] = stream.tile([P, HALF * P], U8, name="scales", align_bytes=64)
+            nc.vector.quantize_mx(out=codes[s][:].bitcast(FP8X4), scales=scales[s][:], in_=grouped[s][:])
+
+        def multiply(m):
+            s, c = divmod(m, 2)
+            units = slice(c * P, (c + 1) * P)
+            acc[m] = psum_mm.tile([P, HALF * P], F32, name="acc")
+            for repeat in range(MX_REPEATS):
+                nc.tensor.matmul_mx(
+                    out=acc[m][:],
+                    lhsT=w_codes[:, units].bitcast(FP8X4),
+                    lhsT_scale=w_scales[:, units],
+                    rhs=codes[s][:].bitcast(FP8X4),
+                    rhs_scale=scales[s][:],
+                    start=True,
+                    stop=True,
+                )
+
+        def activate(m):
+            c = m % 2
+            hidden[m] = stream.tile([P, HALF * P], F32, name="hidden")
+            nc.scalar.activation(out=hidden[m][:], in_=acc[m][:], func=ACT.Relu, bias=b_col[:, c : c + 1], scale=1.0)
+
+        def turn_out(m):
+            back[m] = psum_out.tile([P, HALF, P], F32, name="back")
+            for q in range(HALF):
+                nc.tensor.transpose(out=back[m][:, q, :], in_=hidden[m][:, q * P : (q + 1) * P], identity=ident[:])
+
+        def collect(m):
+            s, c = divmod(m, 2)
+            units = slice(c * P, (c + 1) * P)
+            if c == 0:
+                result[s] = stream.tile([P, HALF, H], F32, name="result")
+            if m % 4 == 3:
+                nc.vector.tensor_copy(out=result[s][:, :, units], in_=back[m][:])
+            else:
+                nc.scalar.copy(out=result[s][:, :, units], in_=back[m][:])
+            if c == 1:
+                first_step = (s % 2) * HALF
+                nc.sync.dma_start(out=out_rows[:, s // 2, first_step : first_step + HALF, :], in_=result[s][:])
+
+        def if_any(stage, index, count):
+            if 0 <= index < count:
+                stage(index)
+
+        with tc.manual_schedule():
+            for m in range(-10, BANKS + 1):
+                if m % 2 == 0:
+                    n = m // 2
+                    if_any(scale, n + 5, HALVES)
+                    if (n + 5) % 2 == 0:
+                        if_any(copy_v0, (n + 5) // 2, ROW_TILES)
+                    if_any(quantise, n + 1, HALVES)
+                    if_any(combine, n + 4, HALVES)
+                if_any(turn_out, m - 1, BANKS)
+                if_any(turn_in, m + 5, BANKS)
+                if_any(multiply, m + 1, BANKS)
+                if_any(activate, m, BANKS)
+                if_any(gather, m + 4, BANKS)
+                if_any(collect, m - 1, BANKS)

@@ -21,7 +21,7 @@ ROW_TILES = ROWS // P
 HALF = STEPS // 2
 WORDS = D // 2
 H_TILES = H // P
-FIRST_TILES = 4
+LOAD_TILES = 4
 HALVES = 2 * ROW_TILES
 BANKS = 2 * HALVES
 MX_REPEATS = 2
@@ -56,8 +56,8 @@ def tile_directnodecomphyperbolicforecaster_pb_t_kernel(tc, z0, v0t, step_sizes,
         b_rows = consts.tile([P, P], BF16)
         nc.vector.memset(b_rows[:], 0.0)
         nc.sync.dma_start(out=raw_step[:], in_=step_sizes.partition_broadcast(P))
-        for first in range(0, ROW_TILES, FIRST_TILES):
-            tiles = slice(first, first + FIRST_TILES)
+        for first in range(0, ROW_TILES, LOAD_TILES):
+            tiles = slice(first, first + LOAD_TILES)
             nc.sync.dma_start(out=z0_sb[:, tiles, :], in_=z0_rows[:, tiles, :])
             nc.sync.dma_start(out=v0_sb[:, tiles, :], in_=v0_rows[:, tiles, :])
             if first == 0:
@@ -248,12 +248,9 @@ def tile_directnodecomphyperbolicforecaster_pb_t_kernel(tc, z0, v0t, step_sizes,
                 out=grid(beta), in0=grid(log_ratio), scalar=0.5, in1=grid(gain_v), op0=ALU.mult, op1=ALU.mult
             )
 
-        for i in range(FIRST_TILES):
+        for i in range(ROW_TILES):
             row_sums(i)
-        coefficients(0, FIRST_TILES, True)
-        for i in range(FIRST_TILES, ROW_TILES):
-            row_sums(i)
-        coefficients(FIRST_TILES, ROW_TILES - FIRST_TILES, False)
+        coefficients(0, ROW_TILES, True)
 
         scaled_z, v0_psum, tan, turned, grouped, codes, scales = {}, {}, {}, {}, {}, {}, {}
         acc, hidden, back, result = {}, {}, {}, {}

@@ -23,7 +23,7 @@ WORDS = D // 2
 H_TILES = H // P
 LOAD_TILES = 4
 HALVES = 2 * ROW_TILES
-BANKS = 2 * HALVES
+ON_GPSIMD = 3
 MX_REPEATS = 2
 
 EPS = 1e-15
@@ -43,7 +43,7 @@ def tile_directnodecomphyperbolicforecaster_pb_t_kernel(tc, z0, v0t, step_sizes,
         consts = ctx.enter_context(tc.tile_pool(name="consts", bufs=1))
         coef = ctx.enter_context(tc.tile_pool(name="coef", bufs=1))
         unread = ctx.enter_context(tc.tile_pool(name="unread", bufs=4))
-        stream = ctx.enter_context(tc.tile_pool(name="stream", bufs=3))
+        stream = ctx.enter_context(tc.tile_pool(name="stream", bufs=2))
         psum_v0 = ctx.enter_context(tc.psum_pool(name="psum_v0", bufs=2))
         psum_in = ctx.enter_context(tc.psum_pool(name="psum_in", bufs=2))
         psum_mm = ctx.enter_context(tc.psum_pool(name="psum_mm", bufs=2))
@@ -56,17 +56,18 @@ def tile_directnodecomphyperbolicforecaster_pb_t_kernel(tc, z0, v0t, step_sizes,
         b_rows = consts.tile([P, P], BF16)
         nc.vector.memset(b_rows[:], 0.0)
         nc.sync.dma_start(out=raw_step[:], in_=step_sizes.partition_broadcast(P))
-        for first in range(0, ROW_TILES, LOAD_TILES):
-            tiles = slice(first, first + LOAD_TILES)
-            nc.sync.dma_start(out=z0_sb[:, tiles, :], in_=z0_rows[:, tiles, :])
-            nc.sync.dma_start(out=v0_sb[:, tiles, :], in_=v0_rows[:, tiles, :])
-            if first == 0:
-                nc.sync.dma_start(out=w_raw[:], in_=W1.rearrange("(q j) c -> q j c", j=4))
-                nc.sync.dma_start(out=b_rows[0:H_TILES, :], in_=b1.rearrange("(c h) -> c h", c=H_TILES))
+        for x_sb, x_rows in ((v0_sb, v0_rows), (z0_sb, z0_rows)):
+            for first in range(0, ROW_TILES, LOAD_TILES):
+                tiles = slice(first, first + LOAD_TILES)
+                nc.sync.dma_start(out=x_sb[:, tiles, :], in_=x_rows[:, tiles, :])
+        nc.sync.dma_start(out=w_raw[:], in_=W1.rearrange("(q j) c -> q j c", j=4))
+        nc.sync.dma_start(out=b_rows[0:H_TILES, :], in_=b1.rearrange("(c h) -> c h", c=H_TILES))
 
         warm = consts.tile([P, 1], F32)
+        one = consts.tile([P, 1], F32)
         nc.vector.memset(warm[:], 1.0)
-        nc.scalar.activation(out=warm[:], in_=warm[:], func=ACT.Sqrt)
+        nc.vector.memset(one[:], 1.0)
+        nc.scalar.activation(out=warm[:], in_=warm[:], func=ACT.Tanh)
 
         ident = consts.tile([P, P], F32)
         make_identity(nc, ident[:])
@@ -77,19 +78,18 @@ def tile_directnodecomphyperbolicforecaster_pb_t_kernel(tc, z0, v0t, step_sizes,
         for t in range(STEPS):
             nc.vector.memset(step_number[:, t : t + 1], float(t + 1))
 
-        w_grouped = consts.tile([P, H, 4], BF16, align_bytes=64)
-        w_codes = consts.tile([P, H], U32, align_bytes=64)
-        w_scales = consts.tile([P, H], U8, align_bytes=64)
-        nc.vector.tensor_copy(out=w_grouped[:], in_=w_raw[:].rearrange("p j c -> p c j"))
+        def load_table_of(func, after):
+            nc.scalar.activation(out=warm[:], in_=after, func=func)
 
-        b_rows32 = consts.tile([P, P], F32)
-        b_col = consts.tile([P, H_TILES], F32)
-        nc.vector.tensor_copy(out=b_rows32[:], in_=b_rows[:])
-        b_turned = psum_in.tile([P, P], F32, tag="turned")
-        nc.tensor.transpose(out=b_turned[:], in_=b_rows32[:], identity=ident[:])
-        nc.vector.tensor_copy(out=b_col[:], in_=b_turned[:, 0:H_TILES])
-        nc.vector.quantize_mx(
-            out=w_codes[:].bitcast(FP8X4), scales=w_scales[:], in_=w_grouped[:].rearrange("p c j -> p (c j)")
+        step = consts.tile([P, 1], F32)
+        step_t = consts.tile([P, STEPS], F32)
+        step_t_capped = consts.tile([P, STEPS], F32)
+        nc.scalar.activation(out=step[:], in_=raw_step[:], func=ACT.Tanh, scale=0.5)
+        nc.vector.tensor_scalar(out=step[:], in0=step[:], scalar1=0.5, scalar2=0.5, op0=ALU.mult, op1=ALU.add)
+        load_table_of(ACT.Sqrt, step[:])
+        nc.vector.tensor_scalar(out=step_t[:], in0=step_number[:], scalar1=step[:, 0:1], scalar2=None, op0=ALU.mult)
+        nc.vector.tensor_scalar(
+            out=step_t_capped[:], in0=step_t[:], scalar1=1.0 / math.sqrt(EPS), scalar2=None, op0=ALU.mult
         )
 
         x2 = coef.tile([P, ROW_TILES], F32)
@@ -106,35 +106,25 @@ def tile_directnodecomphyperbolicforecaster_pb_t_kernel(tc, z0, v0t, step_sizes,
                 out=products[:], in0=x, scalar=1.0, in1=y, op0=ALU.mult, op1=ALU.mult, accum_out=total
             )
 
-        def row_sums(i):
-            z_i, v_i = z0_sb[:, i, :], v0_sb[:, i, :]
-            scalar_sum_of_squares(z_i, x2[:, i : i + 1])
-            vector_sum_of_products(z_i, v_i, xv[:, i : i + 1])
-            if i < ROW_TILES // 2:
-                vector_sum_of_products(v_i, v_i, vv[:, i : i + 1])
-            else:
-                scalar_sum_of_squares(v_i, vv[:, i : i + 1])
-
         def row_tile(name):
             return coef.tile([P, ROW_TILES], F32, name=name)
 
         def grid_tile(name):
             return coef.tile([P, ROW_TILES, STEPS], F32, name=name)
 
-        step = consts.tile([P, 1], F32)
-        step_t = consts.tile([P, STEPS], F32)
-        step_t_capped = consts.tile([P, STEPS], F32)
-        one_minus_x2 = row_tile("one_minus_x2")
-        half_lambda = row_tile("half_lambda")
         vv_floor = row_tile("vv_floor")
         root_vv = row_tile("root_vv")
         newton_row = row_tile("newton_row")
         inv_root_vv = row_tile("inv_root_vv")
+        one_minus_x2 = row_tile("one_minus_x2")
+        half_lambda = row_tile("half_lambda")
+        two_xv = row_tile("two_xv")
         norm_v = grid_tile("norm_v")
         tanh_arg = grid_tile("tanh_arg")
         tanh_val = grid_tile("tanh_val")
+        least_slope = grid_tile("least_slope")
         y_over_v = grid_tile("y_over_v")
-        xy = grid_tile("xy")
+        two_xy = grid_tile("two_xy")
         y2 = grid_tile("y2")
         two_xy_y2 = grid_tile("two_xy_y2")
         den = grid_tile("den")
@@ -142,10 +132,9 @@ def tile_directnodecomphyperbolicforecaster_pb_t_kernel(tc, z0, v0t, step_sizes,
         norm2_m = grid_tile("norm2_m")
         norm_m = grid_tile("norm_m")
         newton = grid_tile("newton")
-        inv_norm_m = grid_tile("inv_norm_m")
         norm_z = grid_tile("norm_z")
-        one_plus = grid_tile("one_plus")
-        one_minus = grid_tile("one_minus")
+        log_plus = grid_tile("log_plus")
+        log_minus = grid_tile("log_minus")
         log_ratio = grid_tile("log_ratio")
         gain = grid_tile("gain")
         gain_z = grid_tile("gain_z")
@@ -153,155 +142,149 @@ def tile_directnodecomphyperbolicforecaster_pb_t_kernel(tc, z0, v0t, step_sizes,
         alpha = grid_tile("alpha")
         beta = grid_tile("beta")
 
-        def load_table_of(func, after):
-            nc.scalar.activation(out=warm[:], in_=after, func=func)
+        def over_steps(x):
+            return x[:].unsqueeze(2).to_broadcast([P, ROW_TILES, STEPS])
 
-        def step_sizes_times_t():
-            nc.scalar.activation(out=step[:], in_=raw_step[:], func=ACT.Tanh, scale=0.5)
-            nc.vector.tensor_scalar(out=step[:], in0=step[:], scalar1=0.5, scalar2=0.5, op0=ALU.mult, op1=ALU.add)
-            nc.vector.tensor_scalar(out=step_t[:], in0=step_number[:], scalar1=step[:, 0:1], scalar2=None, op0=ALU.mult)
-            nc.vector.tensor_scalar(
-                out=step_t_capped[:], in0=step_t[:], scalar1=1.0 / math.sqrt(EPS), scalar2=None, op0=ALU.mult
-            )
+        def over_rows(x):
+            return x[:].unsqueeze(1).to_broadcast([P, ROW_TILES, STEPS])
 
-        def coefficients(first, count, with_step):
-            shape = [P, count, STEPS]
-            v = nc.vector
+        v = nc.vector
 
-            def rows(x):
-                return x[:, first : first + count]
-
-            def grid(x):
-                return x[:, first : first + count, :]
-
-            def over_steps(x):
-                return rows(x).unsqueeze(2).to_broadcast(shape)
-
-            def over_rows(x):
-                return x[:].unsqueeze(1).to_broadcast(shape)
-
-            v.tensor_scalar(out=rows(one_minus_x2), in0=rows(x2), scalar1=-1.0, scalar2=1.0, op0=ALU.mult, op1=ALU.add)
-            v.tensor_scalar_max(out=rows(half_lambda), in0=rows(one_minus_x2), scalar1=EPS)
-            v.reciprocal(out=rows(half_lambda), in_=rows(half_lambda))
-            v.tensor_scalar_max(out=rows(vv_floor), in0=rows(vv), scalar1=TINY)
-            nc.scalar.activation(out=rows(root_vv), in_=rows(vv_floor), func=ACT.Sqrt)
-            load_table_of(ACT.Tanh, root_vv[:, first : first + 1])
-            v.reciprocal(out=rows(newton_row), in_=rows(root_vv))
-            v.scalar_tensor_tensor(
-                out=rows(newton_row), in0=rows(vv_floor), scalar=0.5, in1=rows(newton_row), op0=ALU.mult, op1=ALU.mult
-            )
-            v.scalar_tensor_tensor(
-                out=rows(root_vv), in0=rows(root_vv), scalar=0.5, in1=rows(newton_row), op0=ALU.mult, op1=ALU.add
-            )
-            v.reciprocal(out=rows(inv_root_vv), in_=rows(root_vv))
-            if with_step:
-                step_sizes_times_t()
-            v.tensor_tensor(out=grid(norm_v), in0=over_steps(root_vv), in1=over_rows(step_t), op=ALU.mult)
-            v.scalar_tensor_tensor(
-                out=grid(tanh_arg), in0=grid(norm_v), scalar=math.sqrt(EPS), in1=over_steps(half_lambda),
-                op0=ALU.max, op1=ALU.mult,
-            )
-            nc.scalar.activation(out=grid(tanh_val), in_=grid(tanh_arg), func=ACT.Tanh)
-            load_table_of(ACT.Sqrt, tanh_val[:, first, 0:1])
-            v.tensor_tensor(out=grid(y_over_v), in0=over_steps(inv_root_vv), in1=over_rows(step_t_capped), op=ALU.min)
-            v.tensor_mul(out=grid(y_over_v), in0=grid(y_over_v), in1=grid(tanh_val))
-            v.tensor_tensor(out=grid(xy), in0=grid(y_over_v), in1=over_steps(xv), op=ALU.mult)
-            v.tensor_tensor(out=grid(y2), in0=grid(y_over_v), in1=over_steps(vv), op=ALU.mult)
-            v.tensor_mul(out=grid(y2), in0=grid(y2), in1=grid(y_over_v))
-            v.scalar_tensor_tensor(
-                out=grid(two_xy_y2), in0=grid(xy), scalar=2.0, in1=grid(y2), op0=ALU.mult, op1=ALU.add
-            )
-            v.tensor_tensor(out=grid(den), in0=grid(y2), in1=over_steps(x2), op=ALU.mult)
-            v.scalar_tensor_tensor(out=grid(den), in0=grid(xy), scalar=2.0, in1=grid(den), op0=ALU.mult, op1=ALU.add)
-            v.tensor_scalar(out=grid(den), in0=grid(den), scalar1=1.0, scalar2=EPS, op0=ALU.add, op1=ALU.max)
-            v.reciprocal(out=grid(inv_den), in_=grid(den))
-            v.tensor_tensor(out=grid(norm2_m), in0=grid(two_xy_y2), in1=over_steps(x2), op=ALU.add)
-            v.tensor_mul(out=grid(norm2_m), in0=grid(norm2_m), in1=grid(inv_den))
-            v.tensor_scalar_max(out=grid(norm2_m), in0=grid(norm2_m), scalar1=EPS)
-            nc.scalar.activation(out=grid(norm_m), in_=grid(norm2_m), func=ACT.Sqrt)
-            load_table_of(ACT.Ln, norm2_m[:, first, 0:1])
-            v.reciprocal(out=grid(newton), in_=grid(norm_m))
-            v.scalar_tensor_tensor(
-                out=grid(newton), in0=grid(norm2_m), scalar=0.5, in1=grid(newton), op0=ALU.mult, op1=ALU.mult
-            )
-            v.scalar_tensor_tensor(
-                out=grid(norm_m), in0=grid(norm_m), scalar=0.5, in1=grid(newton), op0=ALU.mult, op1=ALU.add
-            )
-            v.tensor_scalar_min(out=grid(norm_z), in0=grid(norm_m), scalar1=MAXN)
-            v.tensor_scalar(out=grid(one_minus), in0=grid(norm_z), scalar1=-1.0, scalar2=1.0, op0=ALU.mult, op1=ALU.add)
-            v.reciprocal(out=grid(one_minus), in_=grid(one_minus))
-            v.tensor_scalar_add(out=grid(one_plus), in0=grid(norm_z), scalar1=1.0)
-            v.tensor_mul(out=grid(one_plus), in0=grid(one_plus), in1=grid(one_minus))
-            nc.scalar.activation(out=grid(log_ratio), in_=grid(one_plus), func=ACT.Ln)
-            load_table_of(ACT.Sqrt, one_plus[:, first, 0:1])
-            v.reciprocal(out=grid(inv_norm_m), in_=grid(norm_m))
-            v.tensor_mul(out=grid(gain), in0=grid(inv_norm_m), in1=grid(inv_den))
-            v.scalar_tensor_tensor(
-                out=grid(gain_z), in0=grid(two_xy_y2), scalar=1.0, in1=grid(gain), op0=ALU.add, op1=ALU.mult
-            )
-            v.tensor_mul(out=grid(gain_v), in0=grid(y_over_v), in1=grid(gain))
-            v.tensor_tensor(out=grid(gain_v), in0=grid(gain_v), in1=over_steps(one_minus_x2), op=ALU.mult)
-            v.scalar_tensor_tensor(
-                out=grid(alpha), in0=grid(log_ratio), scalar=0.5, in1=grid(gain_z), op0=ALU.mult, op1=ALU.mult
-            )
-            v.scalar_tensor_tensor(
-                out=grid(beta), in0=grid(log_ratio), scalar=0.5, in1=grid(gain_v), op0=ALU.mult, op1=ALU.mult
-            )
+        for i in range(ROW_TILES // 2):
+            vector_sum_of_products(v0_sb[:, i, :], v0_sb[:, i, :], vv[:, i : i + 1])
+            k = ROW_TILES // 2 + i
+            scalar_sum_of_squares(v0_sb[:, k, :], vv[:, k : k + 1])
+        v.tensor_scalar_max(out=vv_floor[:], in0=vv[:], scalar1=TINY)
+        nc.scalar.activation(out=root_vv[:], in_=vv_floor[:], func=ACT.Sqrt)
+        load_table_of(ACT.Tanh, root_vv[:, 0:1])
+        v.reciprocal(out=newton_row[:], in_=root_vv[:])
+        v.scalar_tensor_tensor(
+            out=newton_row[:], in0=vv_floor[:], scalar=0.5, in1=newton_row[:], op0=ALU.mult, op1=ALU.mult
+        )
+        v.scalar_tensor_tensor(
+            out=root_vv[:], in0=root_vv[:], scalar=0.5, in1=newton_row[:], op0=ALU.mult, op1=ALU.add
+        )
+        v.reciprocal(out=inv_root_vv[:], in_=root_vv[:])
+        v.tensor_tensor(out=norm_v[:], in0=over_steps(root_vv), in1=over_rows(step_t), op=ALU.mult)
+        v.tensor_tensor(out=least_slope[:], in0=over_steps(inv_root_vv), in1=over_rows(step_t_capped), op=ALU.min)
 
         for i in range(ROW_TILES):
-            row_sums(i)
-        coefficients(0, ROW_TILES, True)
+            scalar_sum_of_squares(z0_sb[:, i, :], x2[:, i : i + 1])
+        v.tensor_scalar(out=one_minus_x2[:], in0=x2[:], scalar1=-1.0, scalar2=1.0, op0=ALU.mult, op1=ALU.add)
+        v.tensor_scalar_max(out=half_lambda[:], in0=one_minus_x2[:], scalar1=EPS)
+        v.reciprocal(out=half_lambda[:], in_=half_lambda[:])
+        v.scalar_tensor_tensor(
+            out=tanh_arg[:], in0=norm_v[:], scalar=math.sqrt(EPS), in1=over_steps(half_lambda),
+            op0=ALU.max, op1=ALU.mult,
+        )
+        nc.scalar.activation(out=tanh_val[:], in_=tanh_arg[:], func=ACT.Tanh)
+        load_table_of(ACT.Sqrt, tanh_val[:, 0, 0:1])
+
+        for i in range(ROW_TILES):
+            vector_sum_of_products(z0_sb[:, i, :], v0_sb[:, i, :], xv[:, i : i + 1])
+        v.tensor_scalar(out=two_xv[:], in0=xv[:], scalar1=2.0, scalar2=None, op0=ALU.mult)
+        v.tensor_mul(out=y_over_v[:], in0=least_slope[:], in1=tanh_val[:])
+        v.tensor_tensor(out=y2[:], in0=y_over_v[:], in1=over_steps(vv), op=ALU.mult)
+        v.tensor_tensor(out=two_xy[:], in0=y_over_v[:], in1=over_steps(two_xv), op=ALU.mult)
+        v.tensor_mul(out=y2[:], in0=y2[:], in1=y_over_v[:])
+        v.tensor_tensor(out=den[:], in0=y2[:], in1=over_steps(x2), op=ALU.mult)
+        v.tensor_add(out=two_xy_y2[:], in0=two_xy[:], in1=y2[:])
+        v.tensor_add(out=den[:], in0=den[:], in1=two_xy[:])
+        v.tensor_tensor(out=norm2_m[:], in0=two_xy_y2[:], in1=over_steps(x2), op=ALU.add)
+        v.tensor_scalar(out=den[:], in0=den[:], scalar1=1.0, scalar2=EPS, op0=ALU.add, op1=ALU.max)
+        v.tensor_scalar_max(out=norm2_m[:], in0=norm2_m[:], scalar1=TINY)
+        v.reciprocal(out=inv_den[:], in_=den[:])
+        v.tensor_mul(out=norm2_m[:], in0=norm2_m[:], in1=inv_den[:])
+        nc.scalar.activation(out=norm_m[:], in_=norm2_m[:], func=ACT.Sqrt)
+        load_table_of(ACT.Ln, norm_m[:, 0, 0:1])
+        v.reciprocal(out=newton[:], in_=norm_m[:])
+        v.scalar_tensor_tensor(out=newton[:], in0=norm2_m[:], scalar=0.5, in1=newton[:], op0=ALU.mult, op1=ALU.mult)
+        v.scalar_tensor_tensor(out=norm_m[:], in0=norm_m[:], scalar=0.5, in1=newton[:], op0=ALU.mult, op1=ALU.add)
+        v.tensor_scalar_min(out=norm_z[:], in0=norm_m[:], scalar1=MAXN)
+        nc.scalar.activation(out=log_plus[:], in_=norm_z[:], func=ACT.Ln, bias=one[:, 0:1], scale=1.0)
+        nc.scalar.activation(out=log_minus[:], in_=norm_z[:], func=ACT.Ln, bias=one[:, 0:1], scale=-1.0)
+        v.tensor_mul(out=gain[:], in0=norm_m[:], in1=den[:])
+        v.reciprocal(out=gain[:], in_=gain[:])
+        v.scalar_tensor_tensor(
+            out=gain_z[:], in0=two_xy_y2[:], scalar=1.0, in1=gain[:], op0=ALU.add, op1=ALU.mult
+        )
+        v.tensor_mul(out=gain_v[:], in0=y_over_v[:], in1=gain[:])
+        v.tensor_tensor(out=gain_v[:], in0=gain_v[:], in1=over_steps(one_minus_x2), op=ALU.mult)
+        v.tensor_sub(out=log_ratio[:], in0=log_plus[:], in1=log_minus[:])
+        v.scalar_tensor_tensor(
+            out=alpha[:], in0=log_ratio[:], scalar=0.5, in1=gain_z[:], op0=ALU.mult, op1=ALU.mult
+        )
+        v.scalar_tensor_tensor(
+            out=beta[:], in0=log_ratio[:], scalar=0.5, in1=gain_v[:], op0=ALU.mult, op1=ALU.mult
+        )
+
+        w_grouped = consts.tile([P, H, 4], BF16, align_bytes=64)
+        w_codes = consts.tile([P, H], U32, align_bytes=64)
+        w_scales = consts.tile([P, H], U8, align_bytes=64)
+        nc.vector.tensor_copy(out=w_grouped[:], in_=w_raw[:].rearrange("p j c -> p c j"))
+
+        b_rows32 = consts.tile([P, P], F32)
+        b_col = consts.tile([P, H_TILES], F32)
+        nc.vector.tensor_copy(out=b_rows32[:], in_=b_rows[:])
+        b_turned = psum_in.tile([P, P], F32, tag="turned")
+        nc.tensor.transpose(out=b_turned[:], in_=b_rows32[:], identity=ident[:])
+        nc.vector.tensor_copy(out=b_col[:], in_=b_turned[:, 0:H_TILES])
+        nc.vector.quantize_mx(
+            out=w_codes[:].bitcast(FP8X4), scales=w_scales[:], in_=w_grouped[:].rearrange("p c j -> p (c j)")
+        )
 
         scaled_z, v0_psum, tan, turned, grouped, codes, scales = {}, {}, {}, {}, {}, {}, {}
         acc, hidden, back, result = {}, {}, {}, {}
 
-        def scale(s):
-            i = s // 2
-            scaled_z[s] = []
-            for q in range(HALF):
-                t = (s % 2) * HALF + q
-                scaled = stream.tile([P, D], F32, bufs=2 * HALF)
+        def step_of(s, q):
+            return (s % 2) * HALF + q
+
+        def scale(s, q):
+            i, t = s // 2, step_of(s, q)
+            if q < ON_GPSIMD:
+                scaled_z[s, q] = stream.tile([P, D], F32, name="scaled_gpsimd", bufs=ON_GPSIMD)
                 nc.gpsimd.tensor_scalar(
-                    out=scaled[:], in0=z0_sb[:, i, :], scalar1=alpha[:, i, t : t + 1], scalar2=0.0,
+                    out=scaled_z[s, q][:], in0=z0_sb[:, i, :], scalar1=alpha[:, i, t : t + 1], scalar2=0.0,
                     op0=ALU.mult, op1=ALU.add,
                 )
-                scaled_z[s].append(scaled)
+            else:
+                scaled_z[s, q] = stream.tile([P, D], F32, name="scaled_scalar")
+                nc.scalar.activation(
+                    out=scaled_z[s, q][:], in_=z0_sb[:, i, :], func=ACT.Copy, scale=alpha[:, i, t : t + 1]
+                )
 
         def copy_v0(i):
             v0_psum[i] = psum_v0.tile([P, D], F32, name="v0_copy")
             nc.tensor.matmul(out=v0_psum[i][:], lhsT=ident_bf16[:], rhs=v0_sb[:, i, :], start=True, stop=True)
 
-        def combine(s):
-            i = s // 2
-            tan[s] = stream.tile([P, HALF * D], BF16, name="tan")
-            for q in range(HALF):
-                t = (s % 2) * HALF + q
-                nc.vector.scalar_tensor_tensor(
-                    out=tan[s][:, q * D : (q + 1) * D], in0=v0_psum[i][:], scalar=beta[:, i, t : t + 1],
-                    in1=scaled_z[s][q][:], op0=ALU.mult, op1=ALU.add,
-                )
+        def combine(s, q):
+            i, t = s // 2, step_of(s, q)
+            if q == 0:
+                tan[s] = stream.tile([P, HALF * D], BF16, name="tan")
+            nc.vector.scalar_tensor_tensor(
+                out=tan[s][:, q * D : (q + 1) * D], in0=v0_psum[i][:], scalar=beta[:, i, t : t + 1],
+                in1=scaled_z[s, q][:], op0=ALU.mult, op1=ALU.add,
+            )
 
-        def turn_in(m):
-            s, pair = divmod(m, 2)
+        def turn_in(s, pair):
             tan_words = tan[s][:].bitcast(F32)
-            turned[m] = psum_in.tile([P, 2, 2 * P], F32, name="turned", tag="turned")
+            turned[s, pair] = psum_in.tile([P, 2, 2 * P], F32, name="turned", tag="turned")
             for q in range(2):
                 for u in range(2):
                     first_word = (2 * pair + q) * WORDS
                     nc.tensor.transpose(
-                        out=turned[m][:, u, q * P : (q + 1) * P],
+                        out=turned[s, pair][:, u, q * P : (q + 1) * P],
                         in_=tan_words[:, first_word + u : first_word + WORDS : 2],
                         identity=ident[:],
                     )
 
-        def gather(m):
-            s, pair = divmod(m, 2)
+        def gather(s, pair):
             if pair == 0:
                 grouped[s] = stream.tile([P, HALF * P * 4], BF16, name="grouped", align_bytes=64)
             grouped_words = grouped[s][:].bitcast(F32).rearrange("p (c u) -> p c u", u=2)
             nc.scalar.copy(
                 out=grouped_words[:, pair * 2 * P : (pair + 1) * 2 * P, :],
-                in_=turned[m][:].rearrange("p u c -> p c u"),
+                in_=turned[s, pair][:].rearrange("p u c -> p c u"),
             )
 
         def quantise(s):
@@ -309,60 +292,70 @@ def tile_directnodecomphyperbolicforecaster_pb_t_kernel(tc, z0, v0t, step_sizes,
             scales[s] = stream.tile([P, HALF * P], U8, name="scales", align_bytes=64)
             nc.vector.quantize_mx(out=codes[s][:].bitcast(FP8X4), scales=scales[s][:], in_=grouped[s][:])
 
-        def multiply(m):
-            s, c = divmod(m, 2)
-            units = slice(c * P, (c + 1) * P)
-            acc[m] = psum_mm.tile([P, HALF * P], F32, name="acc")
-            for repeat in range(MX_REPEATS):
-                nc.tensor.matmul_mx(
-                    out=acc[m][:],
-                    lhsT=w_codes[:, units].bitcast(FP8X4),
-                    lhsT_scale=w_scales[:, units],
-                    rhs=codes[s][:].bitcast(FP8X4),
-                    rhs_scale=scales[s][:],
-                    start=True,
-                    stop=True,
+        def multiply(s):
+            for c in range(H_TILES):
+                units = slice(c * P, (c + 1) * P)
+                acc[s, c] = psum_mm.tile([P, HALF * P], F32, name="acc")
+                for repeat in range(MX_REPEATS):
+                    nc.tensor.matmul_mx(
+                        out=acc[s, c][:],
+                        lhsT=w_codes[:, units].bitcast(FP8X4),
+                        lhsT_scale=w_scales[:, units],
+                        rhs=codes[s][:].bitcast(FP8X4),
+                        rhs_scale=scales[s][:],
+                        start=True,
+                        stop=True,
+                    )
+
+        def activate(s, c):
+            hidden[s, c] = stream.tile([P, HALF * P], F32, name="hidden")
+            nc.scalar.activation(
+                out=hidden[s, c][:], in_=acc[s, c][:], func=ACT.Relu, bias=b_col[:, c : c + 1], scale=1.0
+            )
+
+        def turn_out(s, c):
+            back[s, c] = psum_out.tile([P, HALF, P], F32, name="back")
+            for q in range(HALF):
+                nc.tensor.transpose(
+                    out=back[s, c][:, q, :], in_=hidden[s, c][:, q * P : (q + 1) * P], identity=ident[:]
                 )
 
-        def activate(m):
-            c = m % 2
-            hidden[m] = stream.tile([P, HALF * P], F32, name="hidden")
-            nc.scalar.activation(out=hidden[m][:], in_=acc[m][:], func=ACT.Relu, bias=b_col[:, c : c + 1], scale=1.0)
-
-        def turn_out(m):
-            back[m] = psum_out.tile([P, HALF, P], F32, name="back")
-            for q in range(HALF):
-                nc.tensor.transpose(out=back[m][:, q, :], in_=hidden[m][:, q * P : (q + 1) * P], identity=ident[:])
-
-        def collect(m):
-            s, c = divmod(m, 2)
+        def collect(s, c):
             units = slice(c * P, (c + 1) * P)
             if c == 0:
-                result[s] = stream.tile([P, HALF, H], F32, name="result")
-            if m % 4 == 3:
-                nc.vector.tensor_copy(out=result[s][:, :, units], in_=back[m][:])
+                result[s] = stream.tile([P, HALF, H], F32, name="result", bufs=3)
+                nc.scalar.copy(out=result[s][:, :, units], in_=back[s, c][:])
             else:
-                nc.scalar.copy(out=result[s][:, :, units], in_=back[m][:])
-            if c == 1:
-                first_step = (s % 2) * HALF
-                nc.sync.dma_start(out=out_rows[:, s // 2, first_step : first_step + HALF, :], in_=result[s][:])
+                nc.vector.tensor_copy(out=result[s][:, :, units], in_=back[s, c][:])
+                nc.sync.dma_start(out=out_rows[:, s // 2, step_of(s, 0) : step_of(s, 0) + HALF, :], in_=result[s][:])
 
-        def if_any(stage, index, count):
-            if 0 <= index < count:
-                stage(index)
+        def run(stage, s, *which):
+            if 0 <= s < HALVES:
+                stage(s, *which)
 
         with tc.manual_schedule():
-            for m in range(-10, BANKS + 1):
-                if m % 2 == 0:
-                    n = m // 2
-                    if_any(scale, n + 5, HALVES)
-                    if (n + 5) % 2 == 0:
-                        if_any(copy_v0, (n + 5) // 2, ROW_TILES)
-                    if_any(quantise, n + 1, HALVES)
-                    if_any(combine, n + 4, HALVES)
-                if_any(turn_out, m - 1, BANKS)
-                if_any(turn_in, m + 5, BANKS)
-                if_any(multiply, m + 1, BANKS)
-                if_any(activate, m, BANKS)
-                if_any(gather, m + 4, BANKS)
-                if_any(collect, m - 1, BANKS)
+            for n in range(-1, HALVES + 2):
+                if n >= HALVES:
+                    run(quantise, n - 1)
+                run(combine, n, 0)
+                run(combine, n, 1)
+                run(multiply, n - 2)
+                run(turn_in, n, 0)
+                run(activate, n - 2, 0)
+                run(activate, n - 2, 1)
+                run(combine, n, 2)
+                run(combine, n, 3)
+                run(turn_out, n - 2, 0)
+                run(turn_out, n - 2, 1)
+                run(gather, n, 0)
+                run(collect, n - 2, 0)
+                run(scale, n + 1, ON_GPSIMD)
+                run(collect, n - 2, 1)
+                run(turn_in, n, 1)
+                run(gather, n, 1)
+                if n < HALVES:
+                    run(quantise, n - 1)
+                for q in range(ON_GPSIMD):
+                    run(scale, n + 1, q)
+                if (n + 1) % 2 == 0 and n + 1 < HALVES:
+                    copy_v0((n + 1) // 2)

@@ -20,15 +20,17 @@ H = 256
 ROW_TILES = ROWS // P
 HALF = STEPS // 2
 WORDS = D // 2
-H_TILES = H // P
 LOAD_TILES = 4
 HALVES = 2 * ROW_TILES
 ON_GPSIMD = 3
+SCALAR_VV = 8
 MX_REPEATS = 2
 
 EPS = 1e-15
 MAXN = 1.0 - 1e-5
 TINY = 1e-30
+
+NUM2_FLOOR = 1e-22
 
 FLOPS = 2 * ROWS * STEPS * D * H
 
@@ -53,15 +55,15 @@ def tile_directnodecomphyperbolicforecaster_pb_t_kernel(tc, z0, v0t, step_sizes,
         v0_sb = consts.tile([P, ROW_TILES, D], BF16)
         raw_step = consts.tile([P, 1], BF16)
         w_raw = consts.tile([P, 4, H], BF16)
-        b_rows = consts.tile([P, P], BF16)
-        nc.vector.memset(b_rows[:], 0.0)
+        b_row = consts.tile([P, H], BF16)
+        nc.vector.memset(b_row[:], 0.0)
         nc.sync.dma_start(out=raw_step[:], in_=step_sizes.partition_broadcast(P))
-        for x_sb, x_rows in ((v0_sb, v0_rows), (z0_sb, z0_rows)):
-            for first in range(0, ROW_TILES, LOAD_TILES):
-                tiles = slice(first, first + LOAD_TILES)
-                nc.sync.dma_start(out=x_sb[:, tiles, :], in_=x_rows[:, tiles, :])
+        for first in range(0, ROW_TILES, LOAD_TILES):
+            tiles = slice(first, first + LOAD_TILES)
+            nc.sync.dma_start(out=v0_sb[:, tiles, :], in_=v0_rows[:, tiles, :])
+            nc.sync.dma_start(out=z0_sb[:, tiles, :], in_=z0_rows[:, tiles, :])
         nc.sync.dma_start(out=w_raw[:], in_=W1.rearrange("(q j) c -> q j c", j=4))
-        nc.sync.dma_start(out=b_rows[0:H_TILES, :], in_=b1.rearrange("(c h) -> c h", c=H_TILES))
+        nc.sync.dma_start(out=b_row[0:1, :], in_=b1.rearrange("(c h) -> c h", c=1))
 
         warm = consts.tile([P, 1], F32)
         one = consts.tile([P, 1], F32)
@@ -117,21 +119,26 @@ def tile_directnodecomphyperbolicforecaster_pb_t_kernel(tc, z0, v0t, step_sizes,
         newton_row = row_tile("newton_row")
         inv_root_vv = row_tile("inv_root_vv")
         one_minus_x2 = row_tile("one_minus_x2")
-        half_lambda = row_tile("half_lambda")
-        two_xv = row_tile("two_xv")
+        minus_half_lambda = row_tile("minus_half_lambda")
         norm_v = grid_tile("norm_v")
-        tanh_arg = grid_tile("tanh_arg")
+        minus_tanh_arg = grid_tile("minus_tanh_arg")
         tanh_val = grid_tile("tanh_val")
+        tanh2 = grid_tile("tanh2")
         least_slope = grid_tile("least_slope")
+        least_y2 = grid_tile("least_y2")
+        least_x2y2 = grid_tile("least_x2y2")
         y_over_v = grid_tile("y_over_v")
-        two_xy = grid_tile("two_xy")
         y2 = grid_tile("y2")
+        x2y2 = grid_tile("x2y2")
+        xy = grid_tile("xy")
         two_xy_y2 = grid_tile("two_xy_y2")
         den = grid_tile("den")
         inv_den = grid_tile("inv_den")
-        norm2_m = grid_tile("norm2_m")
+        num2 = grid_tile("num2")
+        num2_den = grid_tile("num2_den")
+        root = grid_tile("root")
+        half_norm = grid_tile("half_norm")
         norm_m = grid_tile("norm_m")
-        newton = grid_tile("newton")
         norm_z = grid_tile("norm_z")
         log_plus = grid_tile("log_plus")
         log_minus = grid_tile("log_minus")
@@ -150,13 +157,25 @@ def tile_directnodecomphyperbolicforecaster_pb_t_kernel(tc, z0, v0t, step_sizes,
 
         v = nc.vector
 
-        for i in range(ROW_TILES // 2):
-            vector_sum_of_products(v0_sb[:, i, :], v0_sb[:, i, :], vv[:, i : i + 1])
-            k = ROW_TILES // 2 + i
-            scalar_sum_of_squares(v0_sb[:, k, :], vv[:, k : k + 1])
+        def sum_z0(i):
+            scalar_sum_of_squares(z0_sb[:, i, :], x2[:, i : i + 1])
+
+        def sum_v0(i):
+            if i < SCALAR_VV:
+                scalar_sum_of_squares(v0_sb[:, i, :], vv[:, i : i + 1])
+            else:
+                vector_sum_of_products(v0_sb[:, i, :], v0_sb[:, i, :], vv[:, i : i + 1])
+
+        for first in range(0, ROW_TILES - LOAD_TILES, LOAD_TILES):
+            for i in range(first, first + LOAD_TILES):
+                sum_v0(i)
+            for i in range(first, first + LOAD_TILES):
+                sum_z0(i)
+        for i in range(ROW_TILES - LOAD_TILES, ROW_TILES):
+            sum_v0(i)
+
         v.tensor_scalar_max(out=vv_floor[:], in0=vv[:], scalar1=TINY)
         nc.scalar.activation(out=root_vv[:], in_=vv_floor[:], func=ACT.Sqrt)
-        load_table_of(ACT.Tanh, root_vv[:, 0:1])
         v.reciprocal(out=newton_row[:], in_=root_vv[:])
         v.scalar_tensor_tensor(
             out=newton_row[:], in0=vv_floor[:], scalar=0.5, in1=newton_row[:], op0=ALU.mult, op1=ALU.mult
@@ -164,52 +183,59 @@ def tile_directnodecomphyperbolicforecaster_pb_t_kernel(tc, z0, v0t, step_sizes,
         v.scalar_tensor_tensor(
             out=root_vv[:], in0=root_vv[:], scalar=0.5, in1=newton_row[:], op0=ALU.mult, op1=ALU.add
         )
-        v.reciprocal(out=inv_root_vv[:], in_=root_vv[:])
         v.tensor_tensor(out=norm_v[:], in0=over_steps(root_vv), in1=over_rows(step_t), op=ALU.mult)
-        v.tensor_tensor(out=least_slope[:], in0=over_steps(inv_root_vv), in1=over_rows(step_t_capped), op=ALU.min)
 
-        for i in range(ROW_TILES):
-            scalar_sum_of_squares(z0_sb[:, i, :], x2[:, i : i + 1])
-        v.tensor_scalar(out=one_minus_x2[:], in0=x2[:], scalar1=-1.0, scalar2=1.0, op0=ALU.mult, op1=ALU.add)
-        v.tensor_scalar_max(out=half_lambda[:], in0=one_minus_x2[:], scalar1=EPS)
-        v.reciprocal(out=half_lambda[:], in_=half_lambda[:])
+        for i in range(ROW_TILES - LOAD_TILES, ROW_TILES):
+            sum_z0(i)
+        load_table_of(ACT.Tanh, x2[:, ROW_TILES - 1 : ROW_TILES])
+        v.tensor_scalar(
+            out=minus_half_lambda[:], in0=x2[:], scalar1=1.0, scalar2=-EPS, op0=ALU.subtract, op1=ALU.min
+        )
+        v.reciprocal(out=minus_half_lambda[:], in_=minus_half_lambda[:])
         v.scalar_tensor_tensor(
-            out=tanh_arg[:], in0=norm_v[:], scalar=math.sqrt(EPS), in1=over_steps(half_lambda),
+            out=minus_tanh_arg[:], in0=norm_v[:], scalar=math.sqrt(EPS), in1=over_steps(minus_half_lambda),
             op0=ALU.max, op1=ALU.mult,
         )
-        nc.scalar.activation(out=tanh_val[:], in_=tanh_arg[:], func=ACT.Tanh)
+        nc.scalar.activation(out=tanh_val[:], in_=minus_tanh_arg[:], func=ACT.Tanh, scale=-1.0)
         load_table_of(ACT.Sqrt, tanh_val[:, 0, 0:1])
+        v.reciprocal(out=inv_root_vv[:], in_=root_vv[:])
+        v.tensor_tensor(out=least_slope[:], in0=over_steps(inv_root_vv), in1=over_rows(step_t_capped), op=ALU.min)
+        v.tensor_mul(out=least_y2[:], in0=least_slope[:], in1=least_slope[:])
+        v.tensor_tensor(out=least_y2[:], in0=least_y2[:], in1=over_steps(vv), op=ALU.mult)
+        v.tensor_tensor(out=least_x2y2[:], in0=least_y2[:], in1=over_steps(x2), op=ALU.mult)
+        v.tensor_scalar(out=one_minus_x2[:], in0=x2[:], scalar1=-1.0, scalar2=1.0, op0=ALU.mult, op1=ALU.add)
+        v.tensor_mul(out=tanh2[:], in0=tanh_val[:], in1=tanh_val[:])
+        v.tensor_mul(out=y_over_v[:], in0=least_slope[:], in1=tanh_val[:])
+        v.tensor_mul(out=x2y2[:], in0=least_x2y2[:], in1=tanh2[:])
+        v.tensor_mul(out=y2[:], in0=least_y2[:], in1=tanh2[:])
 
         for i in range(ROW_TILES):
             vector_sum_of_products(z0_sb[:, i, :], v0_sb[:, i, :], xv[:, i : i + 1])
-        v.tensor_scalar(out=two_xv[:], in0=xv[:], scalar1=2.0, scalar2=None, op0=ALU.mult)
-        v.tensor_mul(out=y_over_v[:], in0=least_slope[:], in1=tanh_val[:])
-        v.tensor_tensor(out=y2[:], in0=y_over_v[:], in1=over_steps(vv), op=ALU.mult)
-        v.tensor_tensor(out=two_xy[:], in0=y_over_v[:], in1=over_steps(two_xv), op=ALU.mult)
-        v.tensor_mul(out=y2[:], in0=y2[:], in1=y_over_v[:])
-        v.tensor_tensor(out=den[:], in0=y2[:], in1=over_steps(x2), op=ALU.mult)
-        v.tensor_add(out=two_xy_y2[:], in0=two_xy[:], in1=y2[:])
-        v.tensor_add(out=den[:], in0=den[:], in1=two_xy[:])
-        v.tensor_tensor(out=norm2_m[:], in0=two_xy_y2[:], in1=over_steps(x2), op=ALU.add)
+        v.tensor_tensor(out=xy[:], in0=y_over_v[:], in1=over_steps(xv), op=ALU.mult)
+        v.scalar_tensor_tensor(out=den[:], in0=xy[:], scalar=2.0, in1=x2y2[:], op0=ALU.mult, op1=ALU.add)
+        v.scalar_tensor_tensor(out=two_xy_y2[:], in0=xy[:], scalar=2.0, in1=y2[:], op0=ALU.mult, op1=ALU.add)
         v.tensor_scalar(out=den[:], in0=den[:], scalar1=1.0, scalar2=EPS, op0=ALU.add, op1=ALU.max)
-        v.tensor_scalar_max(out=norm2_m[:], in0=norm2_m[:], scalar1=TINY)
+        v.tensor_tensor(out=num2[:], in0=two_xy_y2[:], in1=over_steps(x2), op=ALU.add)
+        v.scalar_tensor_tensor(
+            out=num2_den[:], in0=num2[:], scalar=NUM2_FLOOR, in1=den[:], op0=ALU.max, op1=ALU.mult
+        )
+        nc.scalar.activation(out=root[:], in_=num2_den[:], func=ACT.Sqrt)
+        load_table_of(ACT.Ln, root[:, 0, 0:1])
         v.reciprocal(out=inv_den[:], in_=den[:])
-        v.tensor_mul(out=norm2_m[:], in0=norm2_m[:], in1=inv_den[:])
-        nc.scalar.activation(out=norm_m[:], in_=norm2_m[:], func=ACT.Sqrt)
-        load_table_of(ACT.Ln, norm_m[:, 0, 0:1])
-        v.reciprocal(out=newton[:], in_=norm_m[:])
-        v.scalar_tensor_tensor(out=newton[:], in0=norm2_m[:], scalar=0.5, in1=newton[:], op0=ALU.mult, op1=ALU.mult)
-        v.scalar_tensor_tensor(out=norm_m[:], in0=norm_m[:], scalar=0.5, in1=newton[:], op0=ALU.mult, op1=ALU.add)
+        v.reciprocal(out=gain[:], in_=root[:])
+        v.scalar_tensor_tensor(out=half_norm[:], in0=root[:], scalar=0.5, in1=inv_den[:], op0=ALU.mult, op1=ALU.mult)
+        v.scalar_tensor_tensor(
+            out=norm_m[:], in0=num2[:], scalar=NUM2_FLOOR, in1=gain[:], op0=ALU.max, op1=ALU.mult
+        )
+        v.scalar_tensor_tensor(out=norm_m[:], in0=norm_m[:], scalar=0.5, in1=half_norm[:], op0=ALU.mult, op1=ALU.add)
         v.tensor_scalar_min(out=norm_z[:], in0=norm_m[:], scalar1=MAXN)
         nc.scalar.activation(out=log_plus[:], in_=norm_z[:], func=ACT.Ln, bias=one[:, 0:1], scale=1.0)
         nc.scalar.activation(out=log_minus[:], in_=norm_z[:], func=ACT.Ln, bias=one[:, 0:1], scale=-1.0)
-        v.tensor_mul(out=gain[:], in0=norm_m[:], in1=den[:])
-        v.reciprocal(out=gain[:], in_=gain[:])
         v.scalar_tensor_tensor(
             out=gain_z[:], in0=two_xy_y2[:], scalar=1.0, in1=gain[:], op0=ALU.add, op1=ALU.mult
         )
-        v.tensor_mul(out=gain_v[:], in0=y_over_v[:], in1=gain[:])
-        v.tensor_tensor(out=gain_v[:], in0=gain_v[:], in1=over_steps(one_minus_x2), op=ALU.mult)
+        v.tensor_tensor(out=gain_v[:], in0=y_over_v[:], in1=over_steps(one_minus_x2), op=ALU.mult)
+        v.tensor_mul(out=gain_v[:], in0=gain_v[:], in1=gain[:])
         v.tensor_sub(out=log_ratio[:], in0=log_plus[:], in1=log_minus[:])
         v.scalar_tensor_tensor(
             out=alpha[:], in0=log_ratio[:], scalar=0.5, in1=gain_z[:], op0=ALU.mult, op1=ALU.mult
@@ -223,18 +249,34 @@ def tile_directnodecomphyperbolicforecaster_pb_t_kernel(tc, z0, v0t, step_sizes,
         w_scales = consts.tile([P, H], U8, align_bytes=64)
         nc.vector.tensor_copy(out=w_grouped[:], in_=w_raw[:].rearrange("p j c -> p c j"))
 
-        b_rows32 = consts.tile([P, P], F32)
-        b_col = consts.tile([P, H_TILES], F32)
-        nc.vector.tensor_copy(out=b_rows32[:], in_=b_rows[:])
-        b_turned = psum_in.tile([P, P], F32, tag="turned")
-        nc.tensor.transpose(out=b_turned[:], in_=b_rows32[:], identity=ident[:])
-        nc.vector.tensor_copy(out=b_col[:], in_=b_turned[:, 0:H_TILES])
         nc.vector.quantize_mx(
             out=w_codes[:].bitcast(FP8X4), scales=w_scales[:], in_=w_grouped[:].rearrange("p c j -> p (c j)")
         )
 
+        b_row32 = consts.tile([P, P], F32)
+        b_col = consts.tile([P, 1], F32)
+        b_rows = consts.tile([P, P], F32)
+        ones = consts.tile([P, P], BF16)
+        nc.vector.memset(ones[:], 1.0)
+        nc.vector.tensor_copy(out=b_row32[:], in_=b_row[:, 0:P])
+        b_turned = psum_in.tile([P, P], F32, tag="turned")
+        nc.tensor.transpose(out=b_turned[:], in_=b_row32[:], identity=ident[:])
+        nc.vector.tensor_copy(out=b_col[:], in_=b_turned[:, 0:1])
+        b_spread = psum_in.tile([P, P], F32, tag="turned")
+        nc.tensor.matmul(out=b_spread[:], lhsT=ones[:], rhs=b_row[:, P:H], start=True, stop=True)
+        nc.vector.tensor_copy(out=b_rows[:], in_=b_spread[:])
+
+        z0_even_odd = consts.tile([P, ROW_TILES, D], BF16)
+        for i in range(ROW_TILES):
+            nc.vector.tensor_copy(
+                out=z0_even_odd[:].bitcast(F32)[:, i, :].rearrange("p (u w) -> p u w", u=2),
+                in_=z0_sb[:].bitcast(F32)[:, i, :].rearrange("p (w u) -> p u w", u=2),
+            )
+
         scaled_z, v0_psum, tan, turned, grouped, codes, scales = {}, {}, {}, {}, {}, {}, {}
-        acc, hidden, back, result = {}, {}, {}, {}
+        acc_units, acc_rows, hidden, back, result = {}, {}, {}, {}, {}
+        units_0 = slice(0, P)
+        units_1 = slice(P, H)
 
         def step_of(s, q):
             return (s % 2) * HALF + q
@@ -244,23 +286,29 @@ def tile_directnodecomphyperbolicforecaster_pb_t_kernel(tc, z0, v0t, step_sizes,
             if q < ON_GPSIMD:
                 scaled_z[s, q] = stream.tile([P, D], F32, name="scaled_gpsimd", bufs=ON_GPSIMD)
                 nc.gpsimd.tensor_scalar(
-                    out=scaled_z[s, q][:], in0=z0_sb[:, i, :], scalar1=alpha[:, i, t : t + 1], scalar2=0.0,
+                    out=scaled_z[s, q][:], in0=z0_even_odd[:, i, :], scalar1=alpha[:, i, t : t + 1], scalar2=0.0,
                     op0=ALU.mult, op1=ALU.add,
                 )
             else:
-                scaled_z[s, q] = stream.tile([P, D], F32, name="scaled_scalar")
+                scaled_z[s, q] = stream.tile([P, D], F32, name="scaled_scalar", bufs=2)
                 nc.scalar.activation(
-                    out=scaled_z[s, q][:], in_=z0_sb[:, i, :], func=ACT.Copy, scale=alpha[:, i, t : t + 1]
+                    out=scaled_z[s, q][:], in_=z0_even_odd[:, i, :], func=ACT.Copy, scale=alpha[:, i, t : t + 1]
                 )
 
         def copy_v0(i):
             v0_psum[i] = psum_v0.tile([P, D], F32, name="v0_copy")
-            nc.tensor.matmul(out=v0_psum[i][:], lhsT=ident_bf16[:], rhs=v0_sb[:, i, :], start=True, stop=True)
+            nc.tensor.matmul(
+                out=v0_psum[i][:],
+                lhsT=ident_bf16[:],
+                rhs=v0_sb[:, i, :].rearrange("p (w u e) -> p u w e", u=2, e=2),
+                start=True,
+                stop=True,
+            )
 
         def combine(s, q):
             i, t = s // 2, step_of(s, q)
             if q == 0:
-                tan[s] = stream.tile([P, HALF * D], BF16, name="tan")
+                tan[s] = stream.tile([P, HALF * D], BF16, name="tan", bufs=3)
             nc.vector.scalar_tensor_tensor(
                 out=tan[s][:, q * D : (q + 1) * D], in0=v0_psum[i][:], scalar=beta[:, i, t : t + 1],
                 in1=scaled_z[s, q][:], op0=ALU.mult, op1=ALU.add,
@@ -271,16 +319,16 @@ def tile_directnodecomphyperbolicforecaster_pb_t_kernel(tc, z0, v0t, step_sizes,
             turned[s, pair] = psum_in.tile([P, 2, 2 * P], F32, name="turned", tag="turned")
             for q in range(2):
                 for u in range(2):
-                    first_word = (2 * pair + q) * WORDS
+                    first_word = (2 * pair + q) * WORDS + u * P
                     nc.tensor.transpose(
                         out=turned[s, pair][:, u, q * P : (q + 1) * P],
-                        in_=tan_words[:, first_word + u : first_word + WORDS : 2],
+                        in_=tan_words[:, first_word : first_word + P],
                         identity=ident[:],
                     )
 
         def gather(s, pair):
             if pair == 0:
-                grouped[s] = stream.tile([P, HALF * P * 4], BF16, name="grouped", align_bytes=64)
+                grouped[s] = stream.tile([P, HALF * P * 4], BF16, name="grouped", bufs=3, align_bytes=64)
             grouped_words = grouped[s][:].bitcast(F32).rearrange("p (c u) -> p c u", u=2)
             nc.scalar.copy(
                 out=grouped_words[:, pair * 2 * P : (pair + 1) * 2 * P, :],
@@ -288,73 +336,87 @@ def tile_directnodecomphyperbolicforecaster_pb_t_kernel(tc, z0, v0t, step_sizes,
             )
 
         def quantise(s):
-            codes[s] = stream.tile([P, HALF * P], U32, name="codes", align_bytes=64)
-            scales[s] = stream.tile([P, HALF * P], U8, name="scales", align_bytes=64)
+            codes[s] = stream.tile([P, HALF * P], U32, name="codes", bufs=3, align_bytes=64)
+            scales[s] = stream.tile([P, HALF * P], U8, name="scales", bufs=3, align_bytes=64)
             nc.vector.quantize_mx(out=codes[s][:].bitcast(FP8X4), scales=scales[s][:], in_=grouped[s][:])
 
-        def multiply(s):
-            for c in range(H_TILES):
-                units = slice(c * P, (c + 1) * P)
-                acc[s, c] = psum_mm.tile([P, HALF * P], F32, name="acc")
-                for repeat in range(MX_REPEATS):
+        def multiply_units(s):
+            acc_units[s] = psum_mm.tile([P, HALF * P], F32, name="acc_units", bufs=1)
+            for repeat in range(MX_REPEATS):
+                nc.tensor.matmul_mx(
+                    out=acc_units[s][:],
+                    lhsT=w_codes[:, units_0].bitcast(FP8X4),
+                    lhsT_scale=w_scales[:, units_0],
+                    rhs=codes[s][:].bitcast(FP8X4),
+                    rhs_scale=scales[s][:],
+                    start=True,
+                    stop=True,
+                )
+
+        def activate_units(s):
+            hidden[s] = stream.tile([P, HALF * P], F32, name="hidden", bufs=2)
+            nc.scalar.activation(out=hidden[s][:], in_=acc_units[s][:], func=ACT.Relu, bias=b_col[:, 0:1], scale=1.0)
+
+        def turn_out(s):
+            back[s] = psum_out.tile([P, HALF, P], F32, name="back", bufs=2)
+            for q in range(HALF):
+                nc.tensor.transpose(out=back[s][:, q, :], in_=hidden[s][:, q * P : (q + 1) * P], identity=ident[:])
+
+        def collect(s):
+            nc.scalar.copy(out=result[s][:, :, units_0], in_=back[s][:])
+            first_step = step_of(s, 0)
+            nc.sync.dma_start(out=out_rows[:, s // 2, first_step : first_step + HALF, :], in_=result[s][:])
+
+        def multiply_rows(s):
+            acc_rows[s] = psum_mm.tile([P, HALF, P], F32, name="acc_rows", bufs=1)
+            for repeat in range(MX_REPEATS):
+                for q in range(HALF):
+                    rows = slice(q * P, (q + 1) * P)
                     nc.tensor.matmul_mx(
-                        out=acc[s, c][:],
-                        lhsT=w_codes[:, units].bitcast(FP8X4),
-                        lhsT_scale=w_scales[:, units],
-                        rhs=codes[s][:].bitcast(FP8X4),
-                        rhs_scale=scales[s][:],
+                        out=acc_rows[s][:, q, :],
+                        lhsT=codes[s][:, rows].bitcast(FP8X4),
+                        lhsT_scale=scales[s][:, rows],
+                        rhs=w_codes[:, units_1].bitcast(FP8X4),
+                        rhs_scale=w_scales[:, units_1],
                         start=True,
                         stop=True,
                     )
 
-        def activate(s, c):
-            hidden[s, c] = stream.tile([P, HALF * P], F32, name="hidden")
-            nc.scalar.activation(
-                out=hidden[s, c][:], in_=acc[s, c][:], func=ACT.Relu, bias=b_col[:, c : c + 1], scale=1.0
+        def add_bias_rows(s):
+            result[s] = stream.tile([P, HALF, H], F32, name="result", bufs=4)
+            nc.vector.tensor_tensor(
+                out=result[s][:, :, units_1],
+                in0=acc_rows[s][:],
+                in1=b_rows[:].unsqueeze(1).to_broadcast([P, HALF, P]),
+                op=ALU.add,
             )
 
-        def turn_out(s, c):
-            back[s, c] = psum_out.tile([P, HALF, P], F32, name="back")
-            for q in range(HALF):
-                nc.tensor.transpose(
-                    out=back[s, c][:, q, :], in_=hidden[s, c][:, q * P : (q + 1) * P], identity=ident[:]
-                )
-
-        def collect(s, c):
-            units = slice(c * P, (c + 1) * P)
-            if c == 0:
-                result[s] = stream.tile([P, HALF, H], F32, name="result", bufs=3)
-                nc.scalar.copy(out=result[s][:, :, units], in_=back[s, c][:])
-            else:
-                nc.vector.tensor_copy(out=result[s][:, :, units], in_=back[s, c][:])
-                nc.sync.dma_start(out=out_rows[:, s // 2, step_of(s, 0) : step_of(s, 0) + HALF, :], in_=result[s][:])
+        def relu_rows(s):
+            nc.scalar.activation(out=result[s][:, :, units_1], in_=result[s][:, :, units_1], func=ACT.Relu)
 
         def run(stage, s, *which):
             if 0 <= s < HALVES:
                 stage(s, *which)
 
         with tc.manual_schedule():
-            for n in range(-1, HALVES + 2):
-                if n >= HALVES:
-                    run(quantise, n - 1)
+            for n in range(-1, HALVES + 4):
                 run(combine, n, 0)
                 run(combine, n, 1)
-                run(multiply, n - 2)
-                run(turn_in, n, 0)
-                run(activate, n - 2, 0)
-                run(activate, n - 2, 1)
+                run(multiply_rows, n - 2)
+                run(turn_in, n - 1, 1)
+                run(gather, n - 1, 1)
+                run(collect, n - 4)
+                run(relu_rows, n - 3)
                 run(combine, n, 2)
                 run(combine, n, 3)
-                run(turn_out, n - 2, 0)
-                run(turn_out, n - 2, 1)
+                run(add_bias_rows, n - 2)
+                run(quantise, n - 1)
+                run(multiply_units, n - 2)
+                run(turn_out, n - 3)
+                run(turn_in, n, 0)
+                run(activate_units, n - 2)
                 run(gather, n, 0)
-                run(collect, n - 2, 0)
                 run(scale, n + 1, ON_GPSIMD)
-                run(collect, n - 2, 1)
-                run(turn_in, n, 1)
-                run(gather, n, 1)
-                if n < HALVES:
-                    run(quantise, n - 1)
                 for q in range(ON_GPSIMD):
                     run(scale, n + 1, q)
                 if (n + 1) % 2 == 0 and n + 1 < HALVES:

@@ -20,9 +20,8 @@ H = 256
 ROW_TILES = ROWS // P
 HALF = STEPS // 2
 WORDS = D // 2
-LOAD_TILES = 4
+LOAD_TILES = 2
 HALVES = 2 * ROW_TILES
-ON_GPSIMD = 3
 SCALAR_VV = 8
 MX_REPEATS = 2
 
@@ -58,12 +57,12 @@ def tile_directnodecomphyperbolicforecaster_pb_t_kernel(tc, z0, v0t, step_sizes,
         b_row = consts.tile([P, H], BF16)
         nc.vector.memset(b_row[:], 0.0)
         nc.sync.dma_start(out=raw_step[:], in_=step_sizes.partition_broadcast(P))
+        nc.sync.dma_start(out=b_row[0:1, :], in_=b1.rearrange("(c h) -> c h", c=1))
         for first in range(0, ROW_TILES, LOAD_TILES):
             tiles = slice(first, first + LOAD_TILES)
             nc.sync.dma_start(out=v0_sb[:, tiles, :], in_=v0_rows[:, tiles, :])
             nc.sync.dma_start(out=z0_sb[:, tiles, :], in_=z0_rows[:, tiles, :])
         nc.sync.dma_start(out=w_raw[:], in_=W1.rearrange("(q j) c -> q j c", j=4))
-        nc.sync.dma_start(out=b_row[0:1, :], in_=b1.rearrange("(c h) -> c h", c=1))
 
         warm = consts.tile([P, 1], F32)
         one = consts.tile([P, 1], F32)
@@ -93,6 +92,19 @@ def tile_directnodecomphyperbolicforecaster_pb_t_kernel(tc, z0, v0t, step_sizes,
         nc.vector.tensor_scalar(
             out=step_t_capped[:], in0=step_t[:], scalar1=1.0 / math.sqrt(EPS), scalar2=None, op0=ALU.mult
         )
+
+        b_row32 = consts.tile([P, P], F32)
+        b_col = consts.tile([P, 1], F32)
+        b_rows = consts.tile([P, P], F32)
+        ones = consts.tile([P, P], BF16)
+        nc.vector.memset(ones[:], 1.0)
+        nc.vector.tensor_copy(out=b_row32[:], in_=b_row[:, 0:P])
+        b_turned = psum_in.tile([P, P], F32, tag="turned")
+        nc.tensor.transpose(out=b_turned[:], in_=b_row32[:], identity=ident[:])
+        nc.vector.tensor_copy(out=b_col[:], in_=b_turned[:, 0:1])
+        b_spread = psum_in.tile([P, P], F32, tag="turned")
+        nc.tensor.matmul(out=b_spread[:], lhsT=ones[:], rhs=b_row[:, P:H], start=True, stop=True)
+        nc.vector.tensor_copy(out=b_rows[:], in_=b_spread[:])
 
         x2 = coef.tile([P, ROW_TILES], F32)
         vv = coef.tile([P, ROW_TILES], F32)
@@ -155,6 +167,14 @@ def tile_directnodecomphyperbolicforecaster_pb_t_kernel(tc, z0, v0t, step_sizes,
         def over_rows(x):
             return x[:].unsqueeze(1).to_broadcast([P, ROW_TILES, STEPS])
 
+        z0_even_odd = consts.tile([P, ROW_TILES, D], BF16)
+
+        def even_words_first(i):
+            nc.scalar.copy(
+                out=z0_even_odd[:].bitcast(F32)[:, i, :].rearrange("p (u w) -> p u w", u=2),
+                in_=z0_sb[:].bitcast(F32)[:, i, :].rearrange("p (w u) -> p u w", u=2),
+            )
+
         v = nc.vector
 
         def sum_z0(i):
@@ -166,13 +186,19 @@ def tile_directnodecomphyperbolicforecaster_pb_t_kernel(tc, z0, v0t, step_sizes,
             else:
                 vector_sum_of_products(v0_sb[:, i, :], v0_sb[:, i, :], vv[:, i : i + 1])
 
-        for first in range(0, ROW_TILES - LOAD_TILES, LOAD_TILES):
-            for i in range(first, first + LOAD_TILES):
+        def sum_z0_v0(i):
+            vector_sum_of_products(z0_sb[:, i, :], v0_sb[:, i, :], xv[:, i : i + 1])
+
+        for first in range(0, ROW_TILES, LOAD_TILES):
+            tiles = range(first, first + LOAD_TILES)
+            for i in tiles:
                 sum_v0(i)
-            for i in range(first, first + LOAD_TILES):
-                sum_z0(i)
-        for i in range(ROW_TILES - LOAD_TILES, ROW_TILES):
-            sum_v0(i)
+            if first + LOAD_TILES < ROW_TILES:
+                for i in tiles:
+                    sum_z0(i)
+            if first < SCALAR_VV:
+                for i in tiles:
+                    sum_z0_v0(i)
 
         v.tensor_scalar_max(out=vv_floor[:], in0=vv[:], scalar1=TINY)
         nc.scalar.activation(out=root_vv[:], in_=vv_floor[:], func=ACT.Sqrt)
@@ -198,6 +224,8 @@ def tile_directnodecomphyperbolicforecaster_pb_t_kernel(tc, z0, v0t, step_sizes,
         )
         nc.scalar.activation(out=tanh_val[:], in_=minus_tanh_arg[:], func=ACT.Tanh, scale=-1.0)
         load_table_of(ACT.Sqrt, tanh_val[:, 0, 0:1])
+        for i in range(ROW_TILES // 2):
+            even_words_first(i)
         v.reciprocal(out=inv_root_vv[:], in_=root_vv[:])
         v.tensor_tensor(out=least_slope[:], in0=over_steps(inv_root_vv), in1=over_rows(step_t_capped), op=ALU.min)
         v.tensor_mul(out=least_y2[:], in0=least_slope[:], in1=least_slope[:])
@@ -209,8 +237,8 @@ def tile_directnodecomphyperbolicforecaster_pb_t_kernel(tc, z0, v0t, step_sizes,
         v.tensor_mul(out=x2y2[:], in0=least_x2y2[:], in1=tanh2[:])
         v.tensor_mul(out=y2[:], in0=least_y2[:], in1=tanh2[:])
 
-        for i in range(ROW_TILES):
-            vector_sum_of_products(z0_sb[:, i, :], v0_sb[:, i, :], xv[:, i : i + 1])
+        for i in range(SCALAR_VV, ROW_TILES):
+            sum_z0_v0(i)
         v.tensor_tensor(out=xy[:], in0=y_over_v[:], in1=over_steps(xv), op=ALU.mult)
         v.scalar_tensor_tensor(out=den[:], in0=xy[:], scalar=2.0, in1=x2y2[:], op0=ALU.mult, op1=ALU.add)
         v.scalar_tensor_tensor(out=two_xy_y2[:], in0=xy[:], scalar=2.0, in1=y2[:], op0=ALU.mult, op1=ALU.add)
@@ -247,31 +275,15 @@ def tile_directnodecomphyperbolicforecaster_pb_t_kernel(tc, z0, v0t, step_sizes,
         w_grouped = consts.tile([P, H, 4], BF16, align_bytes=64)
         w_codes = consts.tile([P, H], U32, align_bytes=64)
         w_scales = consts.tile([P, H], U8, align_bytes=64)
-        nc.vector.tensor_copy(out=w_grouped[:], in_=w_raw[:].rearrange("p j c -> p c j"))
 
-        nc.vector.quantize_mx(
-            out=w_codes[:].bitcast(FP8X4), scales=w_scales[:], in_=w_grouped[:].rearrange("p c j -> p (c j)")
-        )
-
-        b_row32 = consts.tile([P, P], F32)
-        b_col = consts.tile([P, 1], F32)
-        b_rows = consts.tile([P, P], F32)
-        ones = consts.tile([P, P], BF16)
-        nc.vector.memset(ones[:], 1.0)
-        nc.vector.tensor_copy(out=b_row32[:], in_=b_row[:, 0:P])
-        b_turned = psum_in.tile([P, P], F32, tag="turned")
-        nc.tensor.transpose(out=b_turned[:], in_=b_row32[:], identity=ident[:])
-        nc.vector.tensor_copy(out=b_col[:], in_=b_turned[:, 0:1])
-        b_spread = psum_in.tile([P, P], F32, tag="turned")
-        nc.tensor.matmul(out=b_spread[:], lhsT=ones[:], rhs=b_row[:, P:H], start=True, stop=True)
-        nc.vector.tensor_copy(out=b_rows[:], in_=b_spread[:])
-
-        z0_even_odd = consts.tile([P, ROW_TILES, D], BF16)
-        for i in range(ROW_TILES):
-            nc.vector.tensor_copy(
-                out=z0_even_odd[:].bitcast(F32)[:, i, :].rearrange("p (u w) -> p u w", u=2),
-                in_=z0_sb[:].bitcast(F32)[:, i, :].rearrange("p (w u) -> p u w", u=2),
+        def quantise_w():
+            nc.vector.tensor_copy(out=w_grouped[:], in_=w_raw[:].rearrange("p j c -> p c j"))
+            nc.vector.quantize_mx(
+                out=w_codes[:].bitcast(FP8X4), scales=w_scales[:], in_=w_grouped[:].rearrange("p c j -> p (c j)")
             )
+
+        for i in range(ROW_TILES // 2, ROW_TILES):
+            even_words_first(i)
 
         scaled_z, v0_psum, tan, turned, grouped, codes, scales = {}, {}, {}, {}, {}, {}, {}
         acc_units, acc_rows, hidden, back, result = {}, {}, {}, {}, {}
@@ -281,19 +293,27 @@ def tile_directnodecomphyperbolicforecaster_pb_t_kernel(tc, z0, v0t, step_sizes,
         def step_of(s, q):
             return (s % 2) * HALF + q
 
-        def scale(s, q):
-            i, t = s // 2, step_of(s, q)
-            if q < ON_GPSIMD:
-                scaled_z[s, q] = stream.tile([P, D], F32, name="scaled_gpsimd", bufs=ON_GPSIMD)
-                nc.gpsimd.tensor_scalar(
-                    out=scaled_z[s, q][:], in0=z0_even_odd[:, i, :], scalar1=alpha[:, i, t : t + 1], scalar2=0.0,
-                    op0=ALU.mult, op1=ALU.add,
-                )
-            else:
-                scaled_z[s, q] = stream.tile([P, D], F32, name="scaled_scalar", bufs=2)
-                nc.scalar.activation(
-                    out=scaled_z[s, q][:], in_=z0_even_odd[:, i, :], func=ACT.Copy, scale=alpha[:, i, t : t + 1]
-                )
+        def on_scalar(s, q):
+            return q == HALF - 1 or (s == 0 and q == 1)
+
+        def scale_on_scalar(s):
+            for q in range(HALF):
+                if on_scalar(s, q):
+                    i, t = s // 2, step_of(s, q)
+                    scaled_z[s, q] = stream.tile([P, D], F32, name="scaled_scalar", bufs=2)
+                    nc.scalar.activation(
+                        out=scaled_z[s, q][:], in_=z0_even_odd[:, i, :], func=ACT.Copy, scale=alpha[:, i, t : t + 1]
+                    )
+
+        def scale_on_gpsimd(s, gate):
+            for q in range(HALF):
+                if not on_scalar(s, q):
+                    i, t = s // 2, step_of(s, q)
+                    scaled_z[s, q] = stream.tile([P, D], F32, name="scaled_gpsimd", bufs=2 * (HALF - 1))
+                    nc.gpsimd.tensor_scalar(
+                        out=scaled_z[s, q][:], in0=z0_even_odd[:, i, :], scalar1=alpha[:, i, t : t + 1],
+                        scalar2=gate[:, 0:1] if gate is not None and q == 0 else 0.0, op0=ALU.mult, op1=ALU.add,
+                    )
 
         def copy_v0(i):
             v0_psum[i] = psum_v0.tile([P, D], F32, name="v0_copy")
@@ -392,32 +412,47 @@ def tile_directnodecomphyperbolicforecaster_pb_t_kernel(tc, z0, v0t, step_sizes,
             )
 
         def relu_rows(s):
-            nc.scalar.activation(out=result[s][:, :, units_1], in_=result[s][:, :, units_1], func=ACT.Relu)
+            rows = result[s][:, :, units_1]
+            if s < HALVES - 2:
+                nc.scalar.activation(out=rows, in_=rows, func=ACT.Relu)
+            else:
+                nc.vector.tensor_scalar_max(out=rows, in0=rows, scalar1=0.0)
 
         def run(stage, s, *which):
             if 0 <= s < HALVES:
                 stage(s, *which)
 
         with tc.manual_schedule():
-            for n in range(-1, HALVES + 4):
+            copy_v0(0)
+            scale_on_scalar(0)
+            scale_on_gpsimd(0, None)
+            scale_on_gpsimd(1, None)
+            for n in range(HALVES + 4):
                 run(combine, n, 0)
                 run(combine, n, 1)
-                run(multiply_rows, n - 2)
                 run(turn_in, n - 1, 1)
+                run(multiply_rows, n - 2)
+                run(activate_units, n - 3)
                 run(gather, n - 1, 1)
-                run(collect, n - 4)
                 run(relu_rows, n - 3)
+                if n == 1:
+                    quantise_w()
+                if n >= HALVES:
+                    run(quantise, n - 1)
                 run(combine, n, 2)
-                run(combine, n, 3)
                 run(add_bias_rows, n - 2)
-                run(quantise, n - 1)
-                run(multiply_units, n - 2)
+                run(combine, n, 3)
+                gate = None
+                if 1 <= n < HALVES:
+                    quantise(n - 1)
+                    gate = stream.tile([P, 1], F32, name="gate", bufs=2)
+                    nc.vector.memset(gate[:], 0.0)
                 run(turn_out, n - 3)
                 run(turn_in, n, 0)
-                run(activate_units, n - 2)
+                run(multiply_units, n - 2)
                 run(gather, n, 0)
-                run(scale, n + 1, ON_GPSIMD)
-                for q in range(ON_GPSIMD):
-                    run(scale, n + 1, q)
-                if (n + 1) % 2 == 0 and n + 1 < HALVES:
+                run(collect, n - 3)
+                run(scale_on_scalar, n + 1)
+                run(scale_on_gpsimd, n + 2, gate)
+                if n % 2 == 1 and n + 1 < HALVES:
                     copy_v0((n + 1) // 2)

@@ -23,12 +23,15 @@ WORDS = D // 2
 LOAD_TILES = 2
 HALVES = 2 * ROW_TILES
 SCALAR_VV = 8
+SCALAR_X2 = 14
 MX_REPEATS = 2
 
 EPS = 1e-15
 MAXN = 1.0 - 1e-5
 TINY = 1e-30
 
+LATE_X2 = 4
+GROUP = 8
 NUM2_FLOOR = 1e-22
 
 FLOPS = 2 * ROWS * STEPS * D * H
@@ -140,6 +143,7 @@ def tile_directnodecomphyperbolicforecaster_pb_t_kernel(tc, z0, v0t, step_sizes,
         least_y2 = grid_tile("least_y2")
         least_x2y2 = grid_tile("least_x2y2")
         y_over_v = grid_tile("y_over_v")
+        slope_v = grid_tile("slope_v")
         y2 = grid_tile("y2")
         x2y2 = grid_tile("x2y2")
         xy = grid_tile("xy")
@@ -178,7 +182,10 @@ def tile_directnodecomphyperbolicforecaster_pb_t_kernel(tc, z0, v0t, step_sizes,
         v = nc.vector
 
         def sum_z0(i):
-            scalar_sum_of_squares(z0_sb[:, i, :], x2[:, i : i + 1])
+            if i < SCALAR_X2:
+                scalar_sum_of_squares(z0_sb[:, i, :], x2[:, i : i + 1])
+            else:
+                vector_sum_of_products(z0_sb[:, i, :], z0_sb[:, i, :], x2[:, i : i + 1])
 
         def sum_v0(i):
             if i < SCALAR_VV:
@@ -193,7 +200,7 @@ def tile_directnodecomphyperbolicforecaster_pb_t_kernel(tc, z0, v0t, step_sizes,
             tiles = range(first, first + LOAD_TILES)
             for i in tiles:
                 sum_v0(i)
-            if first + LOAD_TILES < ROW_TILES:
+            if first < ROW_TILES - LATE_X2:
                 for i in tiles:
                     sum_z0(i)
             if first < SCALAR_VV:
@@ -211,9 +218,9 @@ def tile_directnodecomphyperbolicforecaster_pb_t_kernel(tc, z0, v0t, step_sizes,
         )
         v.tensor_tensor(out=norm_v[:], in0=over_steps(root_vv), in1=over_rows(step_t), op=ALU.mult)
 
-        for i in range(ROW_TILES - LOAD_TILES, ROW_TILES):
+        for i in range(ROW_TILES - LATE_X2, ROW_TILES):
             sum_z0(i)
-        load_table_of(ACT.Tanh, x2[:, ROW_TILES - 1 : ROW_TILES])
+        load_table_of(ACT.Tanh, x2[:, SCALAR_X2 - 1 : SCALAR_X2])
         v.tensor_scalar(
             out=minus_half_lambda[:], in0=x2[:], scalar1=1.0, scalar2=-EPS, op0=ALU.subtract, op1=ALU.min
         )
@@ -224,7 +231,7 @@ def tile_directnodecomphyperbolicforecaster_pb_t_kernel(tc, z0, v0t, step_sizes,
         )
         nc.scalar.activation(out=tanh_val[:], in_=minus_tanh_arg[:], func=ACT.Tanh, scale=-1.0)
         load_table_of(ACT.Sqrt, tanh_val[:, 0, 0:1])
-        for i in range(ROW_TILES // 2):
+        for i in range(0, 6):
             even_words_first(i)
         v.reciprocal(out=inv_root_vv[:], in_=root_vv[:])
         v.tensor_tensor(out=least_slope[:], in0=over_steps(inv_root_vv), in1=over_rows(step_t_capped), op=ALU.min)
@@ -236,41 +243,71 @@ def tile_directnodecomphyperbolicforecaster_pb_t_kernel(tc, z0, v0t, step_sizes,
         v.tensor_mul(out=y_over_v[:], in0=least_slope[:], in1=tanh_val[:])
         v.tensor_mul(out=x2y2[:], in0=least_x2y2[:], in1=tanh2[:])
         v.tensor_mul(out=y2[:], in0=least_y2[:], in1=tanh2[:])
+        v.tensor_tensor(out=slope_v[:], in0=y_over_v[:], in1=over_steps(one_minus_x2), op=ALU.mult)
 
         for i in range(SCALAR_VV, ROW_TILES):
             sum_z0_v0(i)
-        v.tensor_tensor(out=xy[:], in0=y_over_v[:], in1=over_steps(xv), op=ALU.mult)
-        v.scalar_tensor_tensor(out=den[:], in0=xy[:], scalar=2.0, in1=x2y2[:], op0=ALU.mult, op1=ALU.add)
-        v.scalar_tensor_tensor(out=two_xy_y2[:], in0=xy[:], scalar=2.0, in1=y2[:], op0=ALU.mult, op1=ALU.add)
-        v.tensor_scalar(out=den[:], in0=den[:], scalar1=1.0, scalar2=EPS, op0=ALU.add, op1=ALU.max)
-        v.tensor_tensor(out=num2[:], in0=two_xy_y2[:], in1=over_steps(x2), op=ALU.add)
-        v.scalar_tensor_tensor(
-            out=num2_den[:], in0=num2[:], scalar=NUM2_FLOOR, in1=den[:], op0=ALU.max, op1=ALU.mult
-        )
-        nc.scalar.activation(out=root[:], in_=num2_den[:], func=ACT.Sqrt)
-        load_table_of(ACT.Ln, root[:, 0, 0:1])
-        v.reciprocal(out=inv_den[:], in_=den[:])
-        v.reciprocal(out=gain[:], in_=root[:])
-        v.scalar_tensor_tensor(out=half_norm[:], in0=root[:], scalar=0.5, in1=inv_den[:], op0=ALU.mult, op1=ALU.mult)
-        v.scalar_tensor_tensor(
-            out=norm_m[:], in0=num2[:], scalar=NUM2_FLOOR, in1=gain[:], op0=ALU.max, op1=ALU.mult
-        )
-        v.scalar_tensor_tensor(out=norm_m[:], in0=norm_m[:], scalar=0.5, in1=half_norm[:], op0=ALU.mult, op1=ALU.add)
-        v.tensor_scalar_min(out=norm_z[:], in0=norm_m[:], scalar1=MAXN)
-        nc.scalar.activation(out=log_plus[:], in_=norm_z[:], func=ACT.Ln, bias=one[:, 0:1], scale=1.0)
-        nc.scalar.activation(out=log_minus[:], in_=norm_z[:], func=ACT.Ln, bias=one[:, 0:1], scale=-1.0)
-        v.scalar_tensor_tensor(
-            out=gain_z[:], in0=two_xy_y2[:], scalar=1.0, in1=gain[:], op0=ALU.add, op1=ALU.mult
-        )
-        v.tensor_tensor(out=gain_v[:], in0=y_over_v[:], in1=over_steps(one_minus_x2), op=ALU.mult)
-        v.tensor_mul(out=gain_v[:], in0=gain_v[:], in1=gain[:])
-        v.tensor_sub(out=log_ratio[:], in0=log_plus[:], in1=log_minus[:])
-        v.scalar_tensor_tensor(
-            out=alpha[:], in0=log_ratio[:], scalar=0.5, in1=gain_z[:], op0=ALU.mult, op1=ALU.mult
-        )
-        v.scalar_tensor_tensor(
-            out=beta[:], in0=log_ratio[:], scalar=0.5, in1=gain_v[:], op0=ALU.mult, op1=ALU.mult
-        )
+
+        def both(stage):
+            for first in range(0, ROW_TILES, GROUP):
+                stage(slice(first, first + GROUP))
+
+        def row_value(x, g):
+            return x[:, g].unsqueeze(2).to_broadcast([P, GROUP, STEPS])
+
+        def alpha_beta():
+            both(lambda g: v.tensor_tensor(out=xy[:, g, :], in0=y_over_v[:, g, :], in1=row_value(xv, g), op=ALU.mult))
+            both(lambda g: v.scalar_tensor_tensor(
+                out=den[:, g, :], in0=xy[:, g, :], scalar=2.0, in1=x2y2[:, g, :], op0=ALU.mult, op1=ALU.add
+            ))
+            both(lambda g: v.scalar_tensor_tensor(
+                out=two_xy_y2[:, g, :], in0=xy[:, g, :], scalar=2.0, in1=y2[:, g, :], op0=ALU.mult, op1=ALU.add
+            ))
+            both(lambda g: v.tensor_scalar(
+                out=den[:, g, :], in0=den[:, g, :], scalar1=1.0, scalar2=EPS, op0=ALU.add, op1=ALU.max
+            ))
+            both(lambda g: v.tensor_tensor(
+                out=num2[:, g, :], in0=two_xy_y2[:, g, :], in1=row_value(x2, g), op=ALU.add
+            ))
+            both(lambda g: v.scalar_tensor_tensor(
+                out=num2_den[:, g, :], in0=num2[:, g, :], scalar=NUM2_FLOOR, in1=den[:, g, :], op0=ALU.max, op1=ALU.mult
+            ))
+            both(lambda g: nc.scalar.activation(out=root[:, g, :], in_=num2_den[:, g, :], func=ACT.Sqrt))
+            load_table_of(ACT.Ln, root[:, ROW_TILES - 1, 0:1])
+            for i in range(6, 9):
+                even_words_first(i)
+            both(lambda g: v.reciprocal(out=inv_den[:, g, :], in_=den[:, g, :]))
+            both(lambda g: v.reciprocal(out=gain[:, g, :], in_=root[:, g, :]))
+            both(lambda g: v.scalar_tensor_tensor(
+                out=half_norm[:, g, :], in0=root[:, g, :], scalar=0.5, in1=inv_den[:, g, :], op0=ALU.mult, op1=ALU.mult
+            ))
+            both(lambda g: v.scalar_tensor_tensor(
+                out=norm_m[:, g, :], in0=num2[:, g, :], scalar=NUM2_FLOOR, in1=gain[:, g, :], op0=ALU.max, op1=ALU.mult
+            ))
+            both(lambda g: v.scalar_tensor_tensor(
+                out=norm_m[:, g, :], in0=norm_m[:, g, :], scalar=0.5, in1=half_norm[:, g, :], op0=ALU.mult, op1=ALU.add
+            ))
+            both(lambda g: v.tensor_scalar_min(out=norm_z[:, g, :], in0=norm_m[:, g, :], scalar1=MAXN))
+            def logs(g):
+                for sign, log in ((1.0, log_plus), (-1.0, log_minus)):
+                    nc.scalar.activation(
+                        out=log[:, g, :], in_=norm_z[:, g, :], func=ACT.Ln, bias=one[:, 0:1], scale=sign
+                    )
+
+            both(logs)
+            both(lambda g: v.scalar_tensor_tensor(
+                out=gain_z[:, g, :], in0=two_xy_y2[:, g, :], scalar=1.0, in1=gain[:, g, :], op0=ALU.add, op1=ALU.mult
+            ))
+            both(lambda g: v.tensor_mul(out=gain_v[:, g, :], in0=slope_v[:, g, :], in1=gain[:, g, :]))
+            both(lambda g: v.tensor_sub(out=log_ratio[:, g, :], in0=log_plus[:, g, :], in1=log_minus[:, g, :]))
+            both(lambda g: v.scalar_tensor_tensor(
+                out=alpha[:, g, :], in0=log_ratio[:, g, :], scalar=0.5, in1=gain_z[:, g, :], op0=ALU.mult, op1=ALU.mult
+            ))
+            both(lambda g: v.scalar_tensor_tensor(
+                out=beta[:, g, :], in0=log_ratio[:, g, :], scalar=0.5, in1=gain_v[:, g, :], op0=ALU.mult, op1=ALU.mult
+            ))
+
+        alpha_beta()
 
         w_grouped = consts.tile([P, H, 4], BF16, align_bytes=64)
         w_codes = consts.tile([P, H], U32, align_bytes=64)
@@ -282,7 +319,7 @@ def tile_directnodecomphyperbolicforecaster_pb_t_kernel(tc, z0, v0t, step_sizes,
                 out=w_codes[:].bitcast(FP8X4), scales=w_scales[:], in_=w_grouped[:].rearrange("p c j -> p (c j)")
             )
 
-        for i in range(ROW_TILES // 2, ROW_TILES):
+        for i in range(9, ROW_TILES):
             even_words_first(i)
 
         scaled_z, v0_psum, tan, turned, grouped, codes, scales = {}, {}, {}, {}, {}, {}, {}
@@ -294,7 +331,7 @@ def tile_directnodecomphyperbolicforecaster_pb_t_kernel(tc, z0, v0t, step_sizes,
             return (s % 2) * HALF + q
 
         def on_scalar(s, q):
-            return q == HALF - 1 or (s == 0 and q == 1)
+            return q in (0, 2) if s == 0 else q == HALF - 1
 
         def scale_on_scalar(s):
             for q in range(HALF):
@@ -305,14 +342,19 @@ def tile_directnodecomphyperbolicforecaster_pb_t_kernel(tc, z0, v0t, step_sizes,
                         out=scaled_z[s, q][:], in_=z0_even_odd[:, i, :], func=ACT.Copy, scale=alpha[:, i, t : t + 1]
                     )
 
-        def scale_on_gpsimd(s, gate):
+        def scale_on_gpsimd(s):
             for q in range(HALF):
                 if not on_scalar(s, q):
                     i, t = s // 2, step_of(s, q)
-                    scaled_z[s, q] = stream.tile([P, D], F32, name="scaled_gpsimd", bufs=2 * (HALF - 1))
+                    if q == 0:
+                        scaled_z[s, q] = stream.tile(
+                            [P, D], F32, name="scaled_first", tag="grouped", bufs=3, align_bytes=64
+                        )
+                    else:
+                        scaled_z[s, q] = stream.tile([P, D], F32, name="scaled_gpsimd", bufs=4)
                     nc.gpsimd.tensor_scalar(
-                        out=scaled_z[s, q][:], in0=z0_even_odd[:, i, :], scalar1=alpha[:, i, t : t + 1],
-                        scalar2=gate[:, 0:1] if gate is not None and q == 0 else 0.0, op0=ALU.mult, op1=ALU.add,
+                        out=scaled_z[s, q][:], in0=z0_even_odd[:, i, :], scalar1=alpha[:, i, t : t + 1], scalar2=0.0,
+                        op0=ALU.mult, op1=ALU.add,
                     )
 
         def copy_v0(i):
@@ -348,7 +390,7 @@ def tile_directnodecomphyperbolicforecaster_pb_t_kernel(tc, z0, v0t, step_sizes,
 
         def gather(s, pair):
             if pair == 0:
-                grouped[s] = stream.tile([P, HALF * P * 4], BF16, name="grouped", bufs=3, align_bytes=64)
+                grouped[s] = stream.tile([P, HALF * P * 4], BF16, name="grouped", tag="grouped", bufs=3, align_bytes=64)
             grouped_words = grouped[s][:].bitcast(F32).rearrange("p (c u) -> p c u", u=2)
             nc.scalar.copy(
                 out=grouped_words[:, pair * 2 * P : (pair + 1) * 2 * P, :],
@@ -360,9 +402,9 @@ def tile_directnodecomphyperbolicforecaster_pb_t_kernel(tc, z0, v0t, step_sizes,
             scales[s] = stream.tile([P, HALF * P], U8, name="scales", bufs=3, align_bytes=64)
             nc.vector.quantize_mx(out=codes[s][:].bitcast(FP8X4), scales=scales[s][:], in_=grouped[s][:])
 
-        def multiply_units(s):
+        def multiply_units(s, repeats=MX_REPEATS):
             acc_units[s] = psum_mm.tile([P, HALF * P], F32, name="acc_units", bufs=1)
-            for repeat in range(MX_REPEATS):
+            for repeat in range(repeats):
                 nc.tensor.matmul_mx(
                     out=acc_units[s][:],
                     lhsT=w_codes[:, units_0].bitcast(FP8X4),
@@ -382,14 +424,19 @@ def tile_directnodecomphyperbolicforecaster_pb_t_kernel(tc, z0, v0t, step_sizes,
             for q in range(HALF):
                 nc.tensor.transpose(out=back[s][:, q, :], in_=hidden[s][:, q * P : (q + 1) * P], identity=ident[:])
 
-        def collect(s):
-            nc.scalar.copy(out=result[s][:, :, units_0], in_=back[s][:])
-            first_step = step_of(s, 0)
-            nc.sync.dma_start(out=out_rows[:, s // 2, first_step : first_step + HALF, :], in_=result[s][:])
+        def collect(s, on_vector=False):
+            copy = nc.vector.tensor_copy if on_vector else nc.scalar.copy
+            copy(out=result[s][:, :, units_0], in_=back[s][:])
 
-        def multiply_rows(s):
+        def store(s, units=slice(0, H)):
+            first_step = step_of(s, 0)
+            nc.sync.dma_start(
+                out=out_rows[:, s // 2, first_step : first_step + HALF, units], in_=result[s][:, :, units]
+            )
+
+        def multiply_rows(s, repeats=MX_REPEATS):
             acc_rows[s] = psum_mm.tile([P, HALF, P], F32, name="acc_rows", bufs=1)
-            for repeat in range(MX_REPEATS):
+            for repeat in range(repeats):
                 for q in range(HALF):
                     rows = slice(q * P, (q + 1) * P)
                     nc.tensor.matmul_mx(
@@ -411,12 +458,12 @@ def tile_directnodecomphyperbolicforecaster_pb_t_kernel(tc, z0, v0t, step_sizes,
                 op=ALU.add,
             )
 
-        def relu_rows(s):
+        def relu_rows(s, on_vector=False):
             rows = result[s][:, :, units_1]
-            if s < HALVES - 2:
-                nc.scalar.activation(out=rows, in_=rows, func=ACT.Relu)
-            else:
+            if on_vector:
                 nc.vector.tensor_scalar_max(out=rows, in0=rows, scalar1=0.0)
+            else:
+                nc.scalar.activation(out=rows, in_=rows, func=ACT.Relu)
 
         def run(stage, s, *which):
             if 0 <= s < HALVES:
@@ -425,11 +472,11 @@ def tile_directnodecomphyperbolicforecaster_pb_t_kernel(tc, z0, v0t, step_sizes,
         with tc.manual_schedule():
             copy_v0(0)
             scale_on_scalar(0)
-            scale_on_gpsimd(0, None)
-            scale_on_gpsimd(1, None)
-            for n in range(HALVES + 4):
-                run(combine, n, 0)
-                run(combine, n, 1)
+            scale_on_gpsimd(0)
+            scale_on_gpsimd(1)
+            for n in range(HALVES):
+                combine(n, 0)
+                combine(n, 1)
                 run(turn_in, n - 1, 1)
                 run(multiply_rows, n - 2)
                 run(activate_units, n - 3)
@@ -437,22 +484,47 @@ def tile_directnodecomphyperbolicforecaster_pb_t_kernel(tc, z0, v0t, step_sizes,
                 run(relu_rows, n - 3)
                 if n == 1:
                     quantise_w()
-                if n >= HALVES:
-                    run(quantise, n - 1)
-                run(combine, n, 2)
+                combine(n, 2)
                 run(add_bias_rows, n - 2)
-                run(combine, n, 3)
-                gate = None
-                if 1 <= n < HALVES:
-                    quantise(n - 1)
-                    gate = stream.tile([P, 1], F32, name="gate", bufs=2)
-                    nc.vector.memset(gate[:], 0.0)
+                combine(n, 3)
+                run(quantise, n - 1)
                 run(turn_out, n - 3)
-                run(turn_in, n, 0)
+                turn_in(n, 0)
                 run(multiply_units, n - 2)
-                run(gather, n, 0)
-                run(collect, n - 3)
+                gather(n, 0)
+                if n < HALVES - 1:
+                    run(collect, n - 3)
+                    run(store, n - 3)
                 run(scale_on_scalar, n + 1)
-                run(scale_on_gpsimd, n + 2, gate)
+                run(scale_on_gpsimd, n + 2)
                 if n % 2 == 1 and n + 1 < HALVES:
                     copy_v0((n + 1) // 2)
+
+            c, b, a = HALVES - 3, HALVES - 2, HALVES - 1
+            turn_in(a, 1)
+            gather(a, 1)
+            collect(c - 1)
+            store(c - 1)
+            activate_units(c)
+            relu_rows(c, on_vector=True)
+            quantise(a)
+            multiply_rows(b, repeats=1)
+            multiply_units(b, repeats=1)
+            turn_out(c)
+            add_bias_rows(b)
+            activate_units(b)
+            collect(c, on_vector=True)
+            store(c)
+            multiply_units(a, repeats=1)
+            multiply_rows(a, repeats=1)
+            turn_out(b)
+            activate_units(a)
+            relu_rows(b, on_vector=True)
+            add_bias_rows(a)
+            collect(b, on_vector=True)
+            store(b)
+            relu_rows(a, on_vector=True)
+            store(a, units_1)
+            turn_out(a)
+            collect(a)
+            store(a, units_0)

@@ -23,7 +23,7 @@ WORDS = D // 2
 LOAD_TILES = 2
 HALVES = 2 * ROW_TILES
 SCALAR_VV = 8
-SCALAR_X2 = 14
+SCALAR_X2 = 15
 MX_REPEATS = 2
 
 EPS = 1e-15
@@ -61,11 +61,11 @@ def tile_directnodecomphyperbolicforecaster_pb_t_kernel(tc, z0, v0t, step_sizes,
         nc.vector.memset(b_row[:], 0.0)
         nc.sync.dma_start(out=raw_step[:], in_=step_sizes.partition_broadcast(P))
         nc.sync.dma_start(out=b_row[0:1, :], in_=b1.rearrange("(c h) -> c h", c=1))
+        nc.sync.dma_start(out=w_raw[:], in_=W1.rearrange("(q j) c -> q j c", j=4))
         for first in range(0, ROW_TILES, LOAD_TILES):
             tiles = slice(first, first + LOAD_TILES)
             nc.sync.dma_start(out=v0_sb[:, tiles, :], in_=v0_rows[:, tiles, :])
             nc.sync.dma_start(out=z0_sb[:, tiles, :], in_=z0_rows[:, tiles, :])
-        nc.sync.dma_start(out=w_raw[:], in_=W1.rearrange("(q j) c -> q j c", j=4))
 
         warm = consts.tile([P, 1], F32)
         one = consts.tile([P, 1], F32)
@@ -94,6 +94,14 @@ def tile_directnodecomphyperbolicforecaster_pb_t_kernel(tc, z0, v0t, step_sizes,
         nc.vector.tensor_scalar(out=step_t[:], in0=step_number[:], scalar1=step[:, 0:1], scalar2=None, op0=ALU.mult)
         nc.vector.tensor_scalar(
             out=step_t_capped[:], in0=step_t[:], scalar1=1.0 / math.sqrt(EPS), scalar2=None, op0=ALU.mult
+        )
+
+        w_grouped = consts.tile([P, H, 4], BF16, align_bytes=64)
+        w_codes = consts.tile([P, H], U32, align_bytes=64)
+        w_scales = consts.tile([P, H], U8, align_bytes=64)
+        nc.vector.tensor_copy(out=w_grouped[:], in_=w_raw[:].rearrange("p j c -> p c j"))
+        nc.vector.quantize_mx(
+            out=w_codes[:].bitcast(FP8X4), scales=w_scales[:], in_=w_grouped[:].rearrange("p c j -> p (c j)")
         )
 
         b_row32 = consts.tile([P, P], F32)
@@ -274,7 +282,7 @@ def tile_directnodecomphyperbolicforecaster_pb_t_kernel(tc, z0, v0t, step_sizes,
             ))
             both(lambda g: nc.scalar.activation(out=root[:, g, :], in_=num2_den[:, g, :], func=ACT.Sqrt))
             load_table_of(ACT.Ln, root[:, ROW_TILES - 1, 0:1])
-            for i in range(6, 9):
+            for i in range(6, 8):
                 even_words_first(i)
             both(lambda g: v.reciprocal(out=inv_den[:, g, :], in_=den[:, g, :]))
             both(lambda g: v.reciprocal(out=gain[:, g, :], in_=root[:, g, :]))
@@ -309,18 +317,6 @@ def tile_directnodecomphyperbolicforecaster_pb_t_kernel(tc, z0, v0t, step_sizes,
 
         alpha_beta()
 
-        w_grouped = consts.tile([P, H, 4], BF16, align_bytes=64)
-        w_codes = consts.tile([P, H], U32, align_bytes=64)
-        w_scales = consts.tile([P, H], U8, align_bytes=64)
-
-        def quantise_w():
-            nc.vector.tensor_copy(out=w_grouped[:], in_=w_raw[:].rearrange("p j c -> p c j"))
-            nc.vector.quantize_mx(
-                out=w_codes[:].bitcast(FP8X4), scales=w_scales[:], in_=w_grouped[:].rearrange("p c j -> p (c j)")
-            )
-
-        for i in range(9, ROW_TILES):
-            even_words_first(i)
 
         scaled_z, v0_psum, tan, turned, grouped, codes, scales = {}, {}, {}, {}, {}, {}, {}
         acc_units, acc_rows, hidden, back, result = {}, {}, {}, {}, {}
@@ -482,8 +478,6 @@ def tile_directnodecomphyperbolicforecaster_pb_t_kernel(tc, z0, v0t, step_sizes,
                 run(activate_units, n - 3)
                 run(gather, n - 1, 1)
                 run(relu_rows, n - 3)
-                if n == 1:
-                    quantise_w()
                 combine(n, 2)
                 run(add_bias_rows, n - 2)
                 combine(n, 3)
@@ -496,6 +490,8 @@ def tile_directnodecomphyperbolicforecaster_pb_t_kernel(tc, z0, v0t, step_sizes,
                     run(collect, n - 3)
                     run(store, n - 3)
                 run(scale_on_scalar, n + 1)
+                for i in range(8 + 3 * n, min(8 + 3 * (n + 1), ROW_TILES)):
+                    even_words_first(i)
                 run(scale_on_gpsimd, n + 2)
                 if n % 2 == 1 and n + 1 < HALVES:
                     copy_v0((n + 1) // 2)
@@ -503,20 +499,20 @@ def tile_directnodecomphyperbolicforecaster_pb_t_kernel(tc, z0, v0t, step_sizes,
             c, b, a = HALVES - 3, HALVES - 2, HALVES - 1
             turn_in(a, 1)
             gather(a, 1)
-            collect(c - 1)
-            store(c - 1)
             activate_units(c)
-            relu_rows(c, on_vector=True)
+            collect(c - 1, on_vector=True)
+            store(c - 1)
             quantise(a)
             multiply_rows(b, repeats=1)
             multiply_units(b, repeats=1)
             turn_out(c)
+            relu_rows(c, on_vector=True)
             add_bias_rows(b)
             activate_units(b)
-            collect(c, on_vector=True)
-            store(c)
             multiply_units(a, repeats=1)
             multiply_rows(a, repeats=1)
+            collect(c, on_vector=True)
+            store(c)
             turn_out(b)
             activate_units(a)
             relu_rows(b, on_vector=True)

@@ -23,7 +23,7 @@ WORDS = D // 2
 LOAD_TILES = 2
 HALVES = 2 * ROW_TILES
 SCALAR_VV = 8
-SCALAR_X2 = 15
+SCALAR_X2 = 14
 MX_REPEATS = 2
 
 EPS = 1e-15
@@ -238,7 +238,8 @@ def tile_directnodecomphyperbolicforecaster_pb_t_kernel(tc, z0, v0t, step_sizes,
             op0=ALU.max, op1=ALU.mult,
         )
         nc.scalar.activation(out=tanh_val[:], in_=minus_tanh_arg[:], func=ACT.Tanh, scale=-1.0)
-        load_table_of(ACT.Sqrt, tanh_val[:, 0, 0:1])
+        nc.scalar.activation(out=tanh2[:], in_=tanh_val[:], func=ACT.Square)
+        load_table_of(ACT.Sqrt, tanh2[:, 0, 0:1])
         for i in range(0, 6):
             even_words_first(i)
         v.reciprocal(out=inv_root_vv[:], in_=root_vv[:])
@@ -247,11 +248,9 @@ def tile_directnodecomphyperbolicforecaster_pb_t_kernel(tc, z0, v0t, step_sizes,
         v.tensor_tensor(out=least_y2[:], in0=least_y2[:], in1=over_steps(vv), op=ALU.mult)
         v.tensor_tensor(out=least_x2y2[:], in0=least_y2[:], in1=over_steps(x2), op=ALU.mult)
         v.tensor_scalar(out=one_minus_x2[:], in0=x2[:], scalar1=-1.0, scalar2=1.0, op0=ALU.mult, op1=ALU.add)
-        v.tensor_mul(out=tanh2[:], in0=tanh_val[:], in1=tanh_val[:])
         v.tensor_mul(out=y_over_v[:], in0=least_slope[:], in1=tanh_val[:])
         v.tensor_mul(out=x2y2[:], in0=least_x2y2[:], in1=tanh2[:])
         v.tensor_mul(out=y2[:], in0=least_y2[:], in1=tanh2[:])
-        v.tensor_tensor(out=slope_v[:], in0=y_over_v[:], in1=over_steps(one_minus_x2), op=ALU.mult)
 
         for i in range(SCALAR_VV, ROW_TILES):
             sum_z0_v0(i)
@@ -268,15 +267,11 @@ def tile_directnodecomphyperbolicforecaster_pb_t_kernel(tc, z0, v0t, step_sizes,
             both(lambda g: v.scalar_tensor_tensor(
                 out=den[:, g, :], in0=xy[:, g, :], scalar=2.0, in1=x2y2[:, g, :], op0=ALU.mult, op1=ALU.add
             ))
-            both(lambda g: v.scalar_tensor_tensor(
-                out=two_xy_y2[:, g, :], in0=xy[:, g, :], scalar=2.0, in1=y2[:, g, :], op0=ALU.mult, op1=ALU.add
-            ))
+            v.scalar_tensor_tensor(out=two_xy_y2[:], in0=xy[:], scalar=2.0, in1=y2[:], op0=ALU.mult, op1=ALU.add)
             both(lambda g: v.tensor_scalar(
                 out=den[:, g, :], in0=den[:, g, :], scalar1=1.0, scalar2=EPS, op0=ALU.add, op1=ALU.max
             ))
-            both(lambda g: v.tensor_tensor(
-                out=num2[:, g, :], in0=two_xy_y2[:, g, :], in1=row_value(x2, g), op=ALU.add
-            ))
+            v.tensor_tensor(out=num2[:], in0=two_xy_y2[:], in1=over_steps(x2), op=ALU.add)
             both(lambda g: v.scalar_tensor_tensor(
                 out=num2_den[:, g, :], in0=num2[:, g, :], scalar=NUM2_FLOOR, in1=den[:, g, :], op0=ALU.max, op1=ALU.mult
             ))
@@ -284,11 +279,11 @@ def tile_directnodecomphyperbolicforecaster_pb_t_kernel(tc, z0, v0t, step_sizes,
             load_table_of(ACT.Ln, root[:, ROW_TILES - 1, 0:1])
             for i in range(6, 8):
                 even_words_first(i)
-            both(lambda g: v.reciprocal(out=inv_den[:, g, :], in_=den[:, g, :]))
+            v.reciprocal(out=inv_den[:], in_=den[:])
             both(lambda g: v.reciprocal(out=gain[:, g, :], in_=root[:, g, :]))
-            both(lambda g: v.scalar_tensor_tensor(
-                out=half_norm[:, g, :], in0=root[:, g, :], scalar=0.5, in1=inv_den[:, g, :], op0=ALU.mult, op1=ALU.mult
-            ))
+            v.scalar_tensor_tensor(
+                out=half_norm[:], in0=root[:], scalar=0.5, in1=inv_den[:], op0=ALU.mult, op1=ALU.mult
+            )
             both(lambda g: v.scalar_tensor_tensor(
                 out=norm_m[:, g, :], in0=num2[:, g, :], scalar=NUM2_FLOOR, in1=gain[:, g, :], op0=ALU.max, op1=ALU.mult
             ))
@@ -303,10 +298,11 @@ def tile_directnodecomphyperbolicforecaster_pb_t_kernel(tc, z0, v0t, step_sizes,
                     )
 
             both(logs)
-            both(lambda g: v.scalar_tensor_tensor(
-                out=gain_z[:, g, :], in0=two_xy_y2[:, g, :], scalar=1.0, in1=gain[:, g, :], op0=ALU.add, op1=ALU.mult
-            ))
-            both(lambda g: v.tensor_mul(out=gain_v[:, g, :], in0=slope_v[:, g, :], in1=gain[:, g, :]))
+            v.tensor_tensor(out=slope_v[:], in0=y_over_v[:], in1=over_steps(one_minus_x2), op=ALU.mult)
+            v.scalar_tensor_tensor(
+                out=gain_z[:], in0=two_xy_y2[:], scalar=1.0, in1=gain[:], op0=ALU.add, op1=ALU.mult
+            )
+            v.tensor_mul(out=gain_v[:], in0=slope_v[:], in1=gain[:])
             both(lambda g: v.tensor_sub(out=log_ratio[:, g, :], in0=log_plus[:, g, :], in1=log_minus[:, g, :]))
             both(lambda g: v.scalar_tensor_tensor(
                 out=alpha[:, g, :], in0=log_ratio[:, g, :], scalar=0.5, in1=gain_z[:, g, :], op0=ALU.mult, op1=ALU.mult
@@ -399,7 +395,10 @@ def tile_directnodecomphyperbolicforecaster_pb_t_kernel(tc, z0, v0t, step_sizes,
             nc.vector.quantize_mx(out=codes[s][:].bitcast(FP8X4), scales=scales[s][:], in_=grouped[s][:])
 
         def multiply_units(s, repeats=MX_REPEATS):
-            acc_units[s] = psum_mm.tile([P, HALF * P], F32, name="acc_units", bufs=1)
+            if s != HALVES - 2:
+                acc_units[s] = psum_mm.tile([P, HALF * P], F32, name="acc_units", bufs=1)
+            else:
+                acc_units[s] = psum_v0.tile([P, HALF * P], F32, name="v0_copy")
             for repeat in range(repeats):
                 nc.tensor.matmul_mx(
                     out=acc_units[s][:],
@@ -510,17 +509,18 @@ def tile_directnodecomphyperbolicforecaster_pb_t_kernel(tc, z0, v0t, step_sizes,
             add_bias_rows(b)
             activate_units(b)
             multiply_units(a, repeats=1)
-            multiply_rows(a, repeats=1)
             collect(c, on_vector=True)
             store(c)
+            relu_rows(b, on_vector=True)
+            store(b, units_1)
             turn_out(b)
             activate_units(a)
-            relu_rows(b, on_vector=True)
+            multiply_rows(a, repeats=1)
             add_bias_rows(a)
-            collect(b, on_vector=True)
-            store(b)
             relu_rows(a, on_vector=True)
             store(a, units_1)
+            collect(b)
+            store(b, units_0)
             turn_out(a)
             collect(a)
             store(a, units_0)

import math
from contextlib import ExitStack

import concourse.mybir as mybir
from concourse.masks import make_identity

F32 = mybir.dt.float32
BF16 = mybir.dt.bfloat16
U32 = mybir.dt.uint32
U8 = mybir.dt.uint8
FP8X4 = mybir.dt.float8_e4m3fn_x4
ACT = mybir.ActivationFunctionType
ALU = mybir.AluOpType

P = 128
ROWS = 2048
D = 512
STEPS = 8
H = 256
ROW_TILES = ROWS // P
HALF = STEPS // 2
WORDS = D // 2
LOAD_TILES = 2
HALVES = 2 * ROW_TILES
SCALAR_VV = 8
SCALAR_X2 = 14
MX_REPEATS = 2

EPS = 1e-15
MAXN = 1.0 - 1e-5
TINY = 1e-30

LATE_X2 = 4
GROUP = 8
NUM2_FLOOR = 1e-22

FLOPS = 2 * ROWS * STEPS * D * H


def tile_directnodecomphyperbolicforecaster_pb_t_kernel(tc, z0, v0t, step_sizes, W1, b1, out):
    nc = tc.nc
    z0_rows = z0.rearrange("(p i) d -> p i d", i=ROW_TILES)
    v0_rows = v0t.rearrange("(p i) d -> p i d", i=ROW_TILES)
    out_rows = out.rearrange("(p i) t h -> p i t h", i=ROW_TILES)

    with ExitStack() as ctx:
        consts = ctx.enter_context(tc.tile_pool(name="consts", bufs=1))
        coef = ctx.enter_context(tc.tile_pool(name="coef", bufs=1))
        unread = ctx.enter_context(tc.tile_pool(name="unread", bufs=4))
        stream = ctx.enter_context(tc.tile_pool(name="stream", bufs=2))
        psum_v0 = ctx.enter_context(tc.psum_pool(name="psum_v0", bufs=2))
        psum_in = ctx.enter_context(tc.psum_pool(name="psum_in", bufs=2))
        psum_mm = ctx.enter_context(tc.psum_pool(name="psum_mm", bufs=2))
        psum_out = ctx.enter_context(tc.psum_pool(name="psum_out", bufs=2))

        z0_sb = consts.tile([P, ROW_TILES, D], BF16)
        v0_sb = consts.tile([P, ROW_TILES, D], BF16)
        raw_step = consts.tile([P, 1], BF16)
        w_raw = consts.tile([P, 4, H], BF16)
        b_row = consts.tile([P, H], BF16)
        nc.vector.memset(b_row[:], 0.0)
        nc.sync.dma_start(out=raw_step[:], in_=step_sizes.partition_broadcast(P))
        nc.sync.dma_start(out=b_row[0:1, :], in_=b1.rearrange("(c h) -> c h", c=1))
        nc.sync.dma_start(out=w_raw[:], in_=W1.rearrange("(q j) c -> q j c", j=4))
        for first in range(0, ROW_TILES, LOAD_TILES):
            tiles = slice(first, first + LOAD_TILES)
            nc.sync.dma_start(out=v0_sb[:, tiles, :], in_=v0_rows[:, tiles, :])
            nc.sync.dma_start(out=z0_sb[:, tiles, :], in_=z0_rows[:, tiles, :])

        warm = consts.tile([P, 1], F32)
        one = consts.tile([P, 1], F32)
        nc.vector.memset(warm[:], 1.0)
        nc.vector.memset(one[:], 1.0)
        nc.scalar.activation(out=warm[:], in_=warm[:], func=ACT.Tanh)

        ident = consts.tile([P, P], F32)
        make_identity(nc, ident[:])
        ident_bf16 = consts.tile([P, P], BF16)
        make_identity(nc, ident_bf16[:])

        step_number = consts.tile([P, STEPS], F32)
        for t in range(STEPS):
            nc.vector.memset(step_number[:, t : t + 1], float(t + 1))

        def load_table_of(func, after):
            nc.scalar.activation(out=warm[:], in_=after, func=func)

        step = consts.tile([P, 1], F32)
        step_t = consts.tile([P, STEPS], F32)
        step_t_capped = consts.tile([P, STEPS], F32)
        nc.scalar.activation(out=step[:], in_=raw_step[:], func=ACT.Tanh, scale=0.5)
        nc.vector.tensor_scalar(out=step[:], in0=step[:], scalar1=0.5, scalar2=0.5, op0=ALU.mult, op1=ALU.add)
        load_table_of(ACT.Sqrt, step[:])
        nc.vector.tensor_scalar(out=step_t[:], in0=step_number[:], scalar1=step[:, 0:1], scalar2=None, op0=ALU.mult)
        nc.vector.tensor_scalar(
            out=step_t_capped[:], in0=step_t[:], scalar1=1.0 / math.sqrt(EPS), scalar2=None, op0=ALU.mult
        )

        w_grouped = consts.tile([P, H, 4], BF16, align_bytes=64)
        w_codes = consts.tile([P, H], U32, align_bytes=64)
        w_scales = consts.tile([P, H], U8, align_bytes=64)
        nc.vector.tensor_copy(out=w_grouped[:], in_=w_raw[:].rearrange("p j c -> p c j"))
        nc.vector.quantize_mx(
            out=w_codes[:].bitcast(FP8X4), scales=w_scales[:], in_=w_grouped[:].rearrange("p c j -> p (c j)")
        )

        b_row32 = consts.tile([P, P], F32)
        b_col = consts.tile([P, 1], F32)
        b_rows = consts.tile([P, P], F32)
        ones = consts.tile([P, P], BF16)
        nc.vector.memset(ones[:], 1.0)
        nc.vector.tensor_copy(out=b_row32[:], in_=b_row[:, 0:P])
        b_turned = psum_in.tile([P, P], F32, tag="turned")
        nc.tensor.transpose(out=b_turned[:], in_=b_row32[:], identity=ident[:])
        nc.vector.tensor_copy(out=b_col[:], in_=b_turned[:, 0:1])
        b_spread = psum_in.tile([P, P], F32, tag="turned")
        nc.tensor.matmul(out=b_spread[:], lhsT=ones[:], rhs=b_row[:, P:H], start=True, stop=True)
        nc.vector.tensor_copy(out=b_rows[:], in_=b_spread[:])

        x2 = coef.tile([P, ROW_TILES], F32)
        vv = coef.tile([P, ROW_TILES], F32)
        xv = coef.tile([P, ROW_TILES], F32)

        def scalar_sum_of_squares(x, total):
            squares = unread.tile([P, D], BF16)
            nc.scalar.activation(out=squares[:], in_=x, func=ACT.Square, accum_out=total)

        def vector_sum_of_products(x, y, total):
            products = unread.tile([P, D], F32)
            nc.vector.scalar_tensor_tensor(
                out=products[:], in0=x, scalar=1.0, in1=y, op0=ALU.mult, op1=ALU.mult, accum_out=total
            )

        def row_tile(name):
            return coef.tile([P, ROW_TILES], F32, name=name)

        def grid_tile(name):
            return coef.tile([P, ROW_TILES, STEPS], F32, name=name)

        vv_floor = row_tile("vv_floor")
        root_vv = row_tile("root_vv")
        newton_row = row_tile("newton_row")
        inv_root_vv = row_tile("inv_root_vv")
        one_minus_x2 = row_tile("one_minus_x2")
        minus_half_lambda = row_tile("minus_half_lambda")
        norm_v = grid_tile("norm_v")
        minus_tanh_arg = grid_tile("minus_tanh_arg")
        tanh_val = grid_tile("tanh_val")
        tanh2 = grid_tile("tanh2")
        least_slope = grid_tile("least_slope")
        least_y2 = grid_tile("least_y2")
        least_x2y2 = grid_tile("least_x2y2")
        y_over_v = grid_tile("y_over_v")
        slope_v = grid_tile("slope_v")
        y2 = grid_tile("y2")
        x2y2 = grid_tile("x2y2")
        xy = grid_tile("xy")
        two_xy_y2 = grid_tile("two_xy_y2")
        den = grid_tile("den")
        inv_den = grid_tile("inv_den")
        num2 = grid_tile("num2")
        num2_den = grid_tile("num2_den")
        root = grid_tile("root")
        half_norm = grid_tile("half_norm")
        norm_m = grid_tile("norm_m")
        norm_z = grid_tile("norm_z")
        log_plus = grid_tile("log_plus")
        log_minus = grid_tile("log_minus")
        log_ratio = grid_tile("log_ratio")
        gain = grid_tile("gain")
        gain_z = grid_tile("gain_z")
        gain_v = grid_tile("gain_v")
        alpha = grid_tile("alpha")
        beta = grid_tile("beta")

        def over_steps(x):
            return x[:].unsqueeze(2).to_broadcast([P, ROW_TILES, STEPS])

        def over_rows(x):
            return x[:].unsqueeze(1).to_broadcast([P, ROW_TILES, STEPS])

        z0_even_odd = consts.tile([P, ROW_TILES, D], BF16)

        def even_words_first(i):
            nc.scalar.copy(
                out=z0_even_odd[:].bitcast(F32)[:, i, :].rearrange("p (u w) -> p u w", u=2),
                in_=z0_sb[:].bitcast(F32)[:, i, :].rearrange("p (w u) -> p u w", u=2),
            )

        v = nc.vector

        def sum_z0(i):
            if i < SCALAR_X2:
                scalar_sum_of_squares(z0_sb[:, i, :], x2[:, i : i + 1])
            else:
                vector_sum_of_products(z0_sb[:, i, :], z0_sb[:, i, :], x2[:, i : i + 1])

        def sum_v0(i):
            if i < SCALAR_VV:
                scalar_sum_of_squares(v0_sb[:, i, :], vv[:, i : i + 1])
            else:
                vector_sum_of_products(v0_sb[:, i, :], v0_sb[:, i, :], vv[:, i : i + 1])

        def sum_z0_v0(i):
            vector_sum_of_products(z0_sb[:, i, :], v0_sb[:, i, :], xv[:, i : i + 1])

        for first in range(0, ROW_TILES, LOAD_TILES):
            tiles = range(first, first + LOAD_TILES)
            for i in tiles:
                sum_v0(i)
            if first < ROW_TILES - LATE_X2:
                for i in tiles:
                    sum_z0(i)
            if first < SCALAR_VV:
                for i in tiles:
                    sum_z0_v0(i)

        v.tensor_scalar_max(out=vv_floor[:], in0=vv[:], scalar1=TINY)
        nc.scalar.activation(out=root_vv[:], in_=vv_floor[:], func=ACT.Sqrt)
        v.reciprocal(out=newton_row[:], in_=root_vv[:])
        v.scalar_tensor_tensor(
            out=newton_row[:], in0=vv_floor[:], scalar=0.5, in1=newton_row[:], op0=ALU.mult, op1=ALU.mult
        )
        v.scalar_tensor_tensor(
            out=root_vv[:], in0=root_vv[:], scalar=0.5, in1=newton_row[:], op0=ALU.mult, op1=ALU.add
        )
        v.tensor_tensor(out=norm_v[:], in0=over_steps(root_vv), in1=over_rows(step_t), op=ALU.mult)

        for i in range(ROW_TILES - LATE_X2, ROW_TILES):
            sum_z0(i)
        load_table_of(ACT.Tanh, x2[:, SCALAR_X2 - 1 : SCALAR_X2])
        v.tensor_scalar(
            out=minus_half_lambda[:], in0=x2[:], scalar1=1.0, scalar2=-EPS, op0=ALU.subtract, op1=ALU.min
        )
        v.reciprocal(out=minus_half_lambda[:], in_=minus_half_lambda[:])
        v.scalar_tensor_tensor(
            out=minus_tanh_arg[:], in0=norm_v[:], scalar=math.sqrt(EPS), in1=over_steps(minus_half_lambda),
            op0=ALU.max, op1=ALU.mult,
        )
        nc.scalar.activation(out=tanh_val[:], in_=minus_tanh_arg[:], func=ACT.Tanh, scale=-1.0)
        nc.scalar.activation(out=tanh2[:], in_=tanh_val[:], func=ACT.Square)
        load_table_of(ACT.Sqrt, tanh2[:, 0, 0:1])
        for i in range(0, 6):
            even_words_first(i)
        v.reciprocal(out=inv_root_vv[:], in_=root_vv[:])
        v.tensor_tensor(out=least_slope[:], in0=over_steps(inv_root_vv), in1=over_rows(step_t_capped), op=ALU.min)
        v.tensor_mul(out=least_y2[:], in0=least_slope[:], in1=least_slope[:])
        v.tensor_tensor(out=least_y2[:], in0=least_y2[:], in1=over_steps(vv), op=ALU.mult)
        v.tensor_tensor(out=least_x2y2[:], in0=least_y2[:], in1=over_steps(x2), op=ALU.mult)
        v.tensor_scalar(out=one_minus_x2[:], in0=x2[:], scalar1=-1.0, scalar2=1.0, op0=ALU.mult, op1=ALU.add)
        v.tensor_mul(out=y_over_v[:], in0=least_slope[:], in1=tanh_val[:])
        v.tensor_mul(out=x2y2[:], in0=least_x2y2[:], in1=tanh2[:])
        v.tensor_mul(out=y2[:], in0=least_y2[:], in1=tanh2[:])

        for i in range(SCALAR_VV, ROW_TILES):
            sum_z0_v0(i)

        def both(stage):
            for first in range(0, ROW_TILES, GROUP):
                stage(slice(first, first + GROUP))

        def row_value(x, g):
            return x[:, g].unsqueeze(2).to_broadcast([P, GROUP, STEPS])

        def alpha_beta():
            both(lambda g: v.tensor_tensor(out=xy[:, g, :], in0=y_over_v[:, g, :], in1=row_value(xv, g), op=ALU.mult))
            both(lambda g: v.scalar_tensor_tensor(
                out=den[:, g, :], in0=xy[:, g, :], scalar=2.0, in1=x2y2[:, g, :], op0=ALU.mult, op1=ALU.add
            ))
            v.scalar_tensor_tensor(out=two_xy_y2[:], in0=xy[:], scalar=2.0, in1=y2[:], op0=ALU.mult, op1=ALU.add)
            both(lambda g: v.tensor_scalar(
                out=den[:, g, :], in0=den[:, g, :], scalar1=1.0, scalar2=EPS, op0=ALU.add, op1=ALU.max
            ))
            v.tensor_tensor(out=num2[:], in0=two_xy_y2[:], in1=over_steps(x2), op=ALU.add)
            both(lambda g: v.scalar_tensor_tensor(
                out=num2_den[:, g, :], in0=num2[:, g, :], scalar=NUM2_FLOOR, in1=den[:, g, :], op0=ALU.max, op1=ALU.mult
            ))
            both(lambda g: nc.scalar.activation(out=root[:, g, :], in_=num2_den[:, g, :], func=ACT.Sqrt))
            load_table_of(ACT.Ln, root[:, ROW_TILES - 1, 0:1])
            for i in range(6, 8):
                even_words_first(i)
            v.reciprocal(out=inv_den[:], in_=den[:])
            both(lambda g: v.reciprocal(out=gain[:, g, :], in_=root[:, g, :]))
            v.scalar_tensor_tensor(
                out=half_norm[:], in0=root[:], scalar=0.5, in1=inv_den[:], op0=ALU.mult, op1=ALU.mult
            )
            both(lambda g: v.scalar_tensor_tensor(
                out=norm_m[:, g, :], in0=num2[:, g, :], scalar=NUM2_FLOOR, in1=gain[:, g, :], op0=ALU.max, op1=ALU.mult
            ))
            both(lambda g: v.scalar_tensor_tensor(
                out=norm_m[:, g, :], in0=norm_m[:, g, :], scalar=0.5, in1=half_norm[:, g, :], op0=ALU.mult, op1=ALU.add
            ))
            both(lambda g: v.tensor_scalar_min(out=norm_z[:, g, :], in0=norm_m[:, g, :], scalar1=MAXN))
            def logs(g):
                for sign, log in ((1.0, log_plus), (-1.0, log_minus)):
                    nc.scalar.activation(
                        out=log[:, g, :], in_=norm_z[:, g, :], func=ACT.Ln, bias=one[:, 0:1], scale=sign
                    )

            both(logs)
            v.tensor_tensor(out=slope_v[:], in0=y_over_v[:], in1=over_steps(one_minus_x2), op=ALU.mult)
            v.scalar_tensor_tensor(
                out=gain_z[:], in0=two_xy_y2[:], scalar=1.0, in1=gain[:], op0=ALU.add, op1=ALU.mult
            )
            v.tensor_mul(out=gain_v[:], in0=slope_v[:], in1=gain[:])
            both(lambda g: v.tensor_sub(out=log_ratio[:, g, :], in0=log_plus[:, g, :], in1=log_minus[:, g, :]))
            both(lambda g: v.scalar_tensor_tensor(
                out=alpha[:, g, :], in0=log_ratio[:, g, :], scalar=0.5, in1=gain_z[:, g, :], op0=ALU.mult, op1=ALU.mult
            ))
            both(lambda g: v.scalar_tensor_tensor(
                out=beta[:, g, :], in0=log_ratio[:, g, :], scalar=0.5, in1=gain_v[:, g, :], op0=ALU.mult, op1=ALU.mult
            ))

        alpha_beta()


        scaled_z, v0_psum, tan, turned, grouped, codes, scales = {}, {}, {}, {}, {}, {}, {}
        acc_units, acc_rows, hidden, back, result = {}, {}, {}, {}, {}
        units_0 = slice(0, P)
        units_1 = slice(P, H)

        def step_of(s, q):
            return (s % 2) * HALF + q

        def on_scalar(s, q):
            return q in (0, 2) if s == 0 else q == HALF - 1

        def scale_on_scalar(s):
            for q in range(HALF):
                if on_scalar(s, q):
                    i, t = s // 2, step_of(s, q)
                    scaled_z[s, q] = stream.tile([P, D], F32, name="scaled_scalar", bufs=2)
                    nc.scalar.activation(
                        out=scaled_z[s, q][:], in_=z0_even_odd[:, i, :], func=ACT.Copy, scale=alpha[:, i, t : t + 1]
                    )

        def scale_on_gpsimd(s):
            for q in range(HALF):
                if not on_scalar(s, q):
                    i, t = s // 2, step_of(s, q)
                    if q == 0:
                        scaled_z[s, q] = stream.tile(
                            [P, D], F32, name="scaled_first", tag="grouped", bufs=3, align_bytes=64
                        )
                    else:
                        scaled_z[s, q] = stream.tile([P, D], F32, name="scaled_gpsimd", bufs=4)
                    nc.gpsimd.tensor_scalar(
                        out=scaled_z[s, q][:], in0=z0_even_odd[:, i, :], scalar1=alpha[:, i, t : t + 1], scalar2=0.0,
                        op0=ALU.mult, op1=ALU.add,
                    )

        def copy_v0(i):
            v0_psum[i] = psum_v0.tile([P, D], F32, name="v0_copy")
            nc.tensor.matmul(
                out=v0_psum[i][:],
                lhsT=ident_bf16[:],
                rhs=v0_sb[:, i, :].rearrange("p (w u e) -> p u w e", u=2, e=2),
                start=True,
                stop=True,
            )

        def combine(s, q):
            i, t = s // 2, step_of(s, q)
            if q == 0:
                tan[s] = stream.tile([P, HALF * D], BF16, name="tan", bufs=3)
            nc.vector.scalar_tensor_tensor(
                out=tan[s][:, q * D : (q + 1) * D], in0=v0_psum[i][:], scalar=beta[:, i, t : t + 1],
                in1=scaled_z[s, q][:], op0=ALU.mult, op1=ALU.add,
            )

        def turn_in(s, pair):
            tan_words = tan[s][:].bitcast(F32)
            turned[s, pair] = psum_in.tile([P, 2, 2 * P], F32, name="turned", tag="turned")
            for q in range(2):
                for u in range(2):
                    first_word = (2 * pair + q) * WORDS + u * P
                    nc.tensor.transpose(
                        out=turned[s, pair][:, u, q * P : (q + 1) * P],
                        in_=tan_words[:, first_word : first_word + P],
                        identity=ident[:],
                    )

        def gather(s, pair):
            if pair == 0:
                grouped[s] = stream.tile([P, HALF * P * 4], BF16, name="grouped", tag="grouped", bufs=3, align_bytes=64)
            grouped_words = grouped[s][:].bitcast(F32).rearrange("p (c u) -> p c u", u=2)
            nc.scalar.copy(
                out=grouped_words[:, pair * 2 * P : (pair + 1) * 2 * P, :],
                in_=turned[s, pair][:].rearrange("p u c -> p c u"),
            )

        def quantise(s):
            codes[s] = stream.tile([P, HALF * P], U32, name="codes", bufs=3, align_bytes=64)
            scales[s] = stream.tile([P, HALF * P], U8, name="scales", bufs=3, align_bytes=64)
            nc.vector.quantize_mx(out=codes[s][:].bitcast(FP8X4), scales=scales[s][:], in_=grouped[s][:])

        def multiply_units(s, repeats=MX_REPEATS):
            if s != HALVES - 2:
                acc_units[s] = psum_mm.tile([P, HALF * P], F32, name="acc_units", bufs=1)
            else:
                acc_units[s] = psum_v0.tile([P, HALF * P], F32, name="v0_copy")
            for repeat in range(repeats):
                nc.tensor.matmul_mx(
                    out=acc_units[s][:],
                    lhsT=w_codes[:, units_0].bitcast(FP8X4),
                    lhsT_scale=w_scales[:, units_0],
                    rhs=codes[s][:].bitcast(FP8X4),
                    rhs_scale=scales[s][:],
                    start=True,
                    stop=True,
                )

        def activate_units(s):
            hidden[s] = stream.tile([P, HALF * P], F32, name="hidden", bufs=2)
            nc.scalar.activation(out=hidden[s][:], in_=acc_units[s][:], func=ACT.Relu, bias=b_col[:, 0:1], scale=1.0)

        def turn_out(s):
            back[s] = psum_out.tile([P, HALF, P], F32, name="back", bufs=2)
            for q in range(HALF):
                nc.tensor.transpose(out=back[s][:, q, :], in_=hidden[s][:, q * P : (q + 1) * P], identity=ident[:])

        def collect(s, on_vector=False):
            copy = nc.vector.tensor_copy if on_vector else nc.scalar.copy
            copy(out=result[s][:, :, units_0], in_=back[s][:])

        def store(s, units=slice(0, H)):
            first_step = step_of(s, 0)
            nc.sync.dma_start(
                out=out_rows[:, s // 2, first_step : first_step + HALF, units], in_=result[s][:, :, units]
            )

        def multiply_rows(s, repeats=MX_REPEATS):
            acc_rows[s] = psum_mm.tile([P, HALF, P], F32, name="acc_rows", bufs=1)
            for repeat in range(repeats):
                for q in range(HALF):
                    rows = slice(q * P, (q + 1) * P)
                    nc.tensor.matmul_mx(
                        out=acc_rows[s][:, q, :],
                        lhsT=codes[s][:, rows].bitcast(FP8X4),
                        lhsT_scale=scales[s][:, rows],
                        rhs=w_codes[:, units_1].bitcast(FP8X4),
                        rhs_scale=w_scales[:, units_1],
                        start=True,
                        stop=True,
                    )

        def add_bias_rows(s):
            result[s] = stream.tile([P, HALF, H], F32, name="result", bufs=4)
            nc.vector.tensor_tensor(
                out=result[s][:, :, units_1],
                in0=acc_rows[s][:],
                in1=b_rows[:].unsqueeze(1).to_broadcast([P, HALF, P]),
                op=ALU.add,
            )

        def relu_rows(s, on_vector=False):
            rows = result[s][:, :, units_1]
            if on_vector:
                nc.vector.tensor_scalar_max(out=rows, in0=rows, scalar1=0.0)
            else:
                nc.scalar.activation(out=rows, in_=rows, func=ACT.Relu)

        def run(stage, s, *which):
            if 0 <= s < HALVES:
                stage(s, *which)

        with tc.manual_schedule():
            copy_v0(0)
            scale_on_scalar(0)
            scale_on_gpsimd(0)
            scale_on_gpsimd(1)
            for n in range(HALVES):
                combine(n, 0)
                combine(n, 1)
                run(turn_in, n - 1, 1)
                run(multiply_rows, n - 2)
                run(activate_units, n - 3)
                run(gather, n - 1, 1)
                run(relu_rows, n - 3)
                combine(n, 2)
                run(add_bias_rows, n - 2)
                combine(n, 3)
                run(quantise, n - 1)
                run(turn_out, n - 3)
                turn_in(n, 0)
                run(multiply_units, n - 2)
                gather(n, 0)
                if n < HALVES - 1:
                    run(collect, n - 3)
                    run(store, n - 3)
                run(scale_on_scalar, n + 1)
                for i in range(8 + 3 * n, min(8 + 3 * (n + 1), ROW_TILES)):
                    even_words_first(i)
                run(scale_on_gpsimd, n + 2)
                if n % 2 == 1 and n + 1 < HALVES:
                    copy_v0((n + 1) // 2)

            c, b, a = HALVES - 3, HALVES - 2, HALVES - 1
            turn_in(a, 1)
            gather(a, 1)
            activate_units(c)
            collect(c - 1, on_vector=True)
            store(c - 1)
            quantise(a)
            multiply_rows(b, repeats=1)
            multiply_units(b, repeats=1)
            turn_out(c)
            relu_rows(c, on_vector=True)
            add_bias_rows(b)
            activate_units(b)
            multiply_units(a, repeats=1)
            collect(c, on_vector=True)
            store(c)
            relu_rows(b, on_vector=True)
            store(b, units_1)
            turn_out(b)
            activate_units(a)
            multiply_rows(a, repeats=1)
            add_bias_rows(a)
            relu_rows(a, on_vector=True)
            store(a, units_1)
            collect(b)
            store(b, units_0)
            turn_out(a)
            collect(a)
            store(a, units_0)
